import numpy as np
import ml_dtypes


def mxq(x, axis, fmt="e4m3"):
    dtype, down = {"e4m3": (ml_dtypes.float8_e4m3fn, 7), "e5m2": (ml_dtypes.float8_e5m2, 14)}[fmt]
    v = np.moveaxis(np.asarray(x, np.float32).astype(ml_dtypes.bfloat16).astype(np.float64), axis, -1)
    blocks = v.reshape(v.shape[:-1] + (-1, 32))
    amax = np.abs(blocks).max(-1, keepdims=True)
    byte = np.maximum(np.where(amax > 0, np.frexp(amax)[1] - 1 + 127, 0) - down, 1)
    scale = np.exp2(byte - 127.0)
    codes = (blocks / scale).astype(np.float32).astype(dtype).astype(np.float64)
    return np.moveaxis((codes * scale).reshape(v.shape), -1, axis)


WIDE = False


def mx_kscale(k):
    if not WIDE:
        return np.ones(k)
    levels = np.array([10, -10, 5, -5, 0])
    a = np.random.permutation(np.resize(levels, k // 512 * 4)).reshape(k // 512, 4)
    idx = np.arange(k)
    return np.exp2(a[idx // 512, idx % 128 // 32])


BF16 = ml_dtypes.bfloat16


def bf(x):
    return np.asarray(x, np.float32).astype(BF16)


def f64(x):
    return np.asarray(x).astype(np.float64)


B, L, D = 16, 512, 128


def setup_inputs():
    t = mx_kscale(L)
    t = t / t.min()
    u = 1.0 / t.max()
    c, h, q = D // 32, D // 2, D // 4
    tr = t[None, :, None]
    sh = np.log(tr) * np.sqrt(D) / c
    x1 = np.random.standard_normal((B, L, D)) * 1.25
    x2 = np.random.standard_normal((B, L, D)) * 1.25
    x1[:, :, :c] = x1[:, :, :c] * u + (1.0 - u)
    x2[:, :, :c] -= sh
    x1[:, :, h:h + q] *= u
    x2[:, :, h:h + q] *= tr
    x2[:, :, c:2 * c] = x2[:, :, c:2 * c] * u + (1.0 - u)
    x1[:, :, c:2 * c] -= sh
    x2[:, :, h + q:] *= u
    x1[:, :, h + q:] *= tr
    return {"x1": bf(x1), "x2": bf(x2)}


def reference(x1, x2):
    x1, x2 = f64(x1), f64(x2)
    scale = 1.0 / np.sqrt(D)
    s = (x1 @ x2.transpose(0, 2, 1)) * scale
    ea = np.exp(s - s.max(-1, keepdims=True))
    out_a = (mxq(ea, 2, "e4m3") @ mxq(x2, 1, "e4m3")) / ea.sum(-1, keepdims=True)
    st = s.transpose(0, 2, 1)
    eb = np.exp(st - st.max(-1, keepdims=True))
    out_b = (mxq(eb, 2, "e4m3") @ mxq(x1, 1, "e4m3")) / eb.sum(-1, keepdims=True)
    return out_a + out_b

@@ -1,0 +1,193 @@
+from contextlib import ExitStack
+
+import concourse.mybir as mybir
+from concourse.masks import make_identity
+
+FP8X4 = mybir.dt.float8_e4m3fn_x4
+BF16 = mybir.dt.bfloat16
+F32 = mybir.dt.float32
+U32 = mybir.dt.uint32
+U8 = mybir.dt.uint8
+ALU = mybir.AluOpType
+ACT = mybir.ActivationFunctionType
+AX = mybir.AxisListType
+
+B, L, D = 16, 512, 128
+P = 128
+NB = L // P
+SCALE = 1.0 / (D ** 0.5)
+FLOPS = 3 * 2 * B * L * L * D
+PIN = False
+
+
+def tile_mutualcrossattention_t_kernel(tc, x1, x2, out):
+    nc = tc.nc
+    with ExitStack() as ctx:
+        keep = ctx.enter_context(tc.tile_pool(name="keep", bufs=1))
+        two = ctx.enter_context(tc.tile_pool(name="two", bufs=2))
+        three = ctx.enter_context(tc.tile_pool(name="three", bufs=3))
+        psum = ctx.enter_context(tc.psum_pool(name="psum", bufs=2))
+
+        xn = keep.tile([P, 2, B, NB, D], BF16, name="xn")
+        cuts = [0, 1, 2, 4, 8, 16]
+        for lo, hi in zip(cuts[:-1], cuts[1:]):
+            nc.sync.dma_start(out=xn[:, 0, lo:hi], in_=x1[lo:hi].rearrange("b (p t) d -> p b t d", t=NB))
+            nc.sync.dma_start(out=xn[:, 1, lo:hi], in_=x2[lo:hi].rearrange("b (p t) d -> p b t d", t=NB))
+
+        ident_b = keep.tile([P, P], BF16, name="ident_b")
+        make_identity(nc, ident_b[:])
+        ident_f = keep.tile([P, P], F32, name="ident_f")
+        make_identity(nc, ident_f[:])
+
+        xw = keep.tile([P, B, 2 * D], U32, name="xw", align_bytes=64)
+        xs = keep.tile([P, B, 2 * D], U8, name="xs", align_bytes=64)
+        nma = keep.tile([P, B, NB], F32, name="nma")
+        nmb = keep.tile([P, B, NB], F32, name="nmb")
+        suma = keep.tile([P, B, NB], F32, name="suma")
+        sumb = keep.tile([P, B, NB], F32, name="sumb")
+        ra = keep.tile([P, B, NB], F32, name="ra")
+        rb = keep.tile([P, B, NB], F32, name="rb")
+
+        xT, xg, sn, ea, eb, half, grouped, words, planes, acc, tmp, osb = {}, {}, {}, {}, {}, {}, {}, {}, {}, {}, {}, {}
+
+        def ok(m):
+            return 0 <= m < B
+
+        def x_transposes(m):
+            xt_ps = psum.tile([P, 2, NB, P], BF16, tag="s", name="xt_ps")
+            for a in range(2):
+                for t in range(NB):
+                    nc.tensor.transpose(out=xt_ps[:, a, t, :], in_=xn[:, a, m, t, :], identity=ident_b[:])
+            xT[m] = three.tile([P, 2, L], BF16, name="xT")
+            nc.vector.tensor_copy(out=xT[m][:], in_=xt_ps[:].rearrange("p a t m -> p a (t m)"))
+
+        def x_regroup(m):
+            xg[m] = two.tile([P, 2, D, NB], BF16, name="xg", align_bytes=64)
+            nc.gpsimd.tensor_scalar(out=xg[m][:], in0=xn[:, :, m].rearrange("p a t d -> p a d t"),
+                                    scalar1=1.0, scalar2=0.0, op0=ALU.mult, op1=ALU.add)
+
+        def x_quantise(m):
+            nc.vector.quantize_mx(out=xw[:, m, :].bitcast(FP8X4), scales=xs[:, m, :],
+                                  in_=xg[m][:].rearrange("p a d t -> p (a d t)"))
+
+        def scores(m, t):
+            if t == 0:
+                sn[m] = three.tile([P, NB, L], F32, name="sn")
+            s_ps = psum.tile([P, L], F32, tag="s", name="s_ps")
+            nc.tensor.matmul(out=s_ps[:], lhsT=xT[m][:, 0, t * P:(t + 1) * P], rhs=xT[m][:, 1, :],
+                             start=True, stop=True)
+            nc.vector.tensor_scalar(out=sn[m][:, t, :], in0=s_ps[:], scalar1=-SCALE, scalar2=None,
+                                    op0=ALU.mult, op1=ALU.min, accum_out=nma[:, m, t:t + 1])
+
+        def exp_a(m, t):
+            if t == 0:
+                ea[m] = three.tile([P, NB, L], BF16, name="ea")
+            nc.scalar.activation(out=ea[m][:, t, :], in_=sn[m][:, t, :], func=ACT.Exp,
+                                 bias=nma[:, m, t:t + 1], scale=-1.0, accum_out=suma[:, m, t:t + 1])
+
+        def scores_t(m, u):
+            st_ps = psum.tile([P, L], F32, tag="st", name="st_ps")
+            for t in range(NB):
+                nc.tensor.transpose(out=st_ps[:, t * P:(t + 1) * P], in_=sn[m][:, t, u * P:(u + 1) * P],
+                                    identity=ident_f[:])
+            nc.vector.tensor_reduce(out=nmb[:, m, u:u + 1], in_=st_ps[:], axis=AX.X, op=ALU.min)
+            return st_ps
+
+        def exp_b(m, u, st_ps):
+            if u == 0:
+                eb[m] = three.tile([P, NB, L], BF16, name="eb")
+            nc.scalar.activation(out=eb[m][:, u, :], in_=st_ps[:], func=ACT.Exp,
+                                 bias=nmb[:, m, u:u + 1], scale=-1.0, accum_out=sumb[:, m, u:u + 1])
+
+        def e_transposes(side, m, h):
+            src = ea[m] if side == 0 else eb[m]
+            et_ps = psum.tile([P, 2, NB, P], BF16, tag="et", name="et_ps")
+            for r in range(2):
+                for c in range(NB):
+                    nc.tensor.transpose(out=et_ps[:, r, c, :], in_=src[:, 2 * h + r, c * P:(c + 1) * P],
+                                        identity=ident_b[:])
+            half[(side, m, h)] = three.tile([P, 2, NB, P], BF16, name="half")
+            nc.scalar.copy(out=half[(side, m, h)][:], in_=et_ps[:])
+
+        def e_regroup(side, m, h):
+            if h == 0:
+                grouped[(side, m)] = two.tile([P, NB, P, NB], BF16, name="grouped%d" % side, align_bytes=64)
+            nc.gpsimd.tensor_scalar(out=grouped[(side, m)][:, 2 * h:2 * h + 2],
+                                    in0=half[(side, m, h)][:].rearrange("p r c m -> p r m c"),
+                                    scalar1=1.0, scalar2=0.0, op0=ALU.mult, op1=ALU.add)
+
+        def e_quantise(side, m):
+            words[(side, m)] = two.tile([P, L], U32, name="words%d" % side, align_bytes=64)
+            planes[(side, m)] = two.tile([P, L], U8, name="planes%d" % side, align_bytes=64)
+            nc.vector.quantize_mx(out=words[(side, m)][:].bitcast(FP8X4), scales=planes[(side, m)][:],
+                                  in_=grouped[(side, m)][:].rearrange("p r m c -> p (r m c)"))
+
+        def products(m):
+            for side in range(2):
+                acc[(side, m)] = psum.tile([P, NB, D], F32, tag="o", name="acc")
+                other = (1 - side) * D
+                for q in range(NB):
+                    nc.tensor.matmul_mx(out=acc[(side, m)][:, q, :],
+                                        lhsT=words[(side, m)][:, q * P:(q + 1) * P].bitcast(FP8X4),
+                                        lhsT_scale=planes[(side, m)][:, q * P:(q + 1) * P],
+                                        rhs=xw[:, m, other:other + D].bitcast(FP8X4),
+                                        rhs_scale=xs[:, m, other:other + D],
+                                        start=True, stop=True)
+            nc.vector.reciprocal(out=ra[:, m, :], in_=suma[:, m, :])
+            nc.vector.reciprocal(out=rb[:, m, :], in_=sumb[:, m, :])
+            tmp[m] = two.tile([P, NB, D], F32, name="tmp")
+            osb[m] = three.tile([P, NB, D], F32, name="osb")
+
+        def finish(m, q):
+            nc.scalar.activation(out=tmp[m][:, q, :], in_=acc[(0, m)][:, q, :], func=ACT.Copy,
+                                 scale=ra[:, m, q:q + 1])
+            nc.vector.scalar_tensor_tensor(out=osb[m][:, q, :], in0=acc[(1, m)][:, q, :],
+                                           scalar=rb[:, m, q:q + 1], in1=tmp[m][:, q, :],
+                                           op0=ALU.mult, op1=ALU.add)
+            if q == NB - 1:
+                nc.sync.dma_start(out=out[m].rearrange("(p q) d -> p q d", q=NB), in_=osb[m][:])
+
+        et_plan = [(0, 1, 0), (1, 2, 1), (0, 1, 1), (1, 1, 0)]
+
+        def quarter(k, q):
+            st_ps = None
+            if ok(k - 1):
+                st_ps = scores_t(k - 1, q)
+            if ok(k):
+                scores(k, q)
+            lag_m, lag_t = (k, q - 1) if q > 0 else (k - 1, NB - 1)
+            if ok(lag_m):
+                exp_a(lag_m, lag_t)
+            if ok(k - 1):
+                exp_b(k - 1, q, st_ps)
+            pk, pq = (k, q - 1) if q > 0 else (k - 1, NB - 1)
+            side, off, h = et_plan[pq]
+            if ok(pk - off):
+                e_regroup(side, pk - off, h)
+            side, off, h = et_plan[q]
+            if ok(k - off):
+                e_transposes(side, k - off, h)
+            if q == 0 and ok(k - 2):
+                e_quantise(0, k - 2)
+            if q == 1 and ok(k - 3):
+                products(k - 3)
+                finish(k - 3, 0)
+                finish(k - 3, 1)
+            if q == 2:
+                if ok(k - 3):
+                    finish(k - 3, 2)
+                    finish(k - 3, 3)
+                if ok(k + 1):
+                    x_transposes(k + 1)
+                    x_regroup(k + 1)
+            if q == 3:
+                if ok(k - 2):
+                    e_quantise(1, k - 2)
+                if ok(k + 1):
+                    x_quantise(k + 1)
+
+        if PIN:
+            ctx.enter_context(tc.manual_schedule())
+        for k in range(-1, B + 4):
+            for q in range(NB):
+                quarter(k, q)

@@ -17,7 +17,8 @@ P = 128
 NB = L // P
 SCALE = 1.0 / (D ** 0.5)
 FLOPS = 3 * 2 * B * L * L * D
-PIN = False
+PIN = True
+NMX = 256
 
 
 def tile_mutualcrossattention_t_kernel(tc, x1, x2, out):
@@ -50,8 +51,13 @@ def tile_mutualcrossattention_t_kernel(tc, x1, x2, out):
 
         xT, xg, sn, ea, eb, half, grouped, words, planes, acc, tmp, osb = {}, {}, {}, {}, {}, {}, {}, {}, {}, {}, {}, {}
 
-        def ok(m):
-            return 0 <= m < B
+        def at(g, first):
+            m, r = divmod(g - first, NB)
+            return m if (r == 0 and 0 <= m < B) else None
+
+        def split(g, first):
+            m, q = divmod(g - first, NB)
+            return (m, q) if 0 <= m < B else None
 
         def x_transposes(m):
             xt_ps = psum.tile([P, 2, NB, P], BF16, tag="s", name="xt_ps")
@@ -61,23 +67,45 @@ def tile_mutualcrossattention_t_kernel(tc, x1, x2, out):
             xT[m] = three.tile([P, 2, L], BF16, name="xT")
             nc.vector.tensor_copy(out=xT[m][:], in_=xt_ps[:].rearrange("p a t m -> p a (t m)"))
 
-        def x_regroup(m):
-            xg[m] = two.tile([P, 2, D, NB], BF16, name="xg", align_bytes=64)
-            nc.gpsimd.tensor_scalar(out=xg[m][:], in0=xn[:, :, m].rearrange("p a t d -> p a d t"),
+        def x_regroup(m, a):
+            if a == 0:
+                xg[m] = two.tile([P, 2, D, NB], BF16, name="xg", align_bytes=64)
+            nc.gpsimd.tensor_scalar(out=xg[m][:, a], in0=xn[:, a, m].rearrange("p t d -> p d t"),
                                     scalar1=1.0, scalar2=0.0, op0=ALU.mult, op1=ALU.add)
 
         def x_quantise(m):
             nc.vector.quantize_mx(out=xw[:, m, :].bitcast(FP8X4), scales=xs[:, m, :],
                                   in_=xg[m][:].rearrange("p a d t -> p (a d t)"))
 
-        def scores(m, t):
-            if t == 0:
-                sn[m] = three.tile([P, NB, L], F32, name="sn")
-            s_ps = psum.tile([P, L], F32, tag="s", name="s_ps")
-            nc.tensor.matmul(out=s_ps[:], lhsT=xT[m][:, 0, t * P:(t + 1) * P], rhs=xT[m][:, 1, :],
-                             start=True, stop=True)
-            nc.vector.tensor_scalar(out=sn[m][:, t, :], in0=s_ps[:], scalar1=-SCALE, scalar2=None,
-                                    op0=ALU.mult, op1=ALU.min, accum_out=nma[:, m, t:t + 1])
+        def products(m, q):
+            acc[(m, q)] = psum.tile([P, 2, NMX], F32, tag="o", name="acc")
+            for side in range(2):
+                lo = 0 if NMX == 2 * D else (1 - side) * D
+                nc.tensor.matmul_mx(out=acc[(m, q)][:, side, :],
+                                    lhsT=words[(side, m)][:, q * P:(q + 1) * P].bitcast(FP8X4),
+                                    lhsT_scale=planes[(side, m)][:, q * P:(q + 1) * P],
+                                    rhs=xw[:, m, lo:lo + NMX].bitcast(FP8X4),
+                                    rhs_scale=xs[:, m, lo:lo + NMX],
+                                    start=True, stop=True)
+
+        def scores_and_products(sc, mx):
+            hw = L // 2
+            s_ps = None
+            if sc is not None:
+                m, t = sc
+                if t == 0:
+                    sn[m] = three.tile([P, NB, L], F32, name="sn")
+                s_ps = psum.tile([P, L], F32, tag="s", name="s_ps")
+                nc.tensor.matmul(out=s_ps[:, 0:hw], lhsT=xT[m][:, 0, t * P:(t + 1) * P], rhs=xT[m][:, 1, 0:hw],
+                                 start=True, stop=True)
+            if mx is not None:
+                products(mx[0], mx[1])
+            if sc is not None:
+                m, t = sc
+                nc.tensor.matmul(out=s_ps[:, hw:L], lhsT=xT[m][:, 0, t * P:(t + 1) * P], rhs=xT[m][:, 1, hw:L],
+                                 start=True, stop=True)
+                nc.vector.tensor_scalar(out=sn[m][:, t, :], in0=s_ps[:], scalar1=-SCALE, scalar2=None,
+                                        op0=ALU.mult, op1=ALU.min, accum_out=nma[:, m, t:t + 1])
 
         def exp_a(m, t):
             if t == 0:
@@ -116,78 +144,74 @@ def tile_mutualcrossattention_t_kernel(tc, x1, x2, out):
                                     in0=half[(side, m, h)][:].rearrange("p r c m -> p r m c"),
                                     scalar1=1.0, scalar2=0.0, op0=ALU.mult, op1=ALU.add)
 
-        def e_quantise(side, m):
-            words[(side, m)] = two.tile([P, L], U32, name="words%d" % side, align_bytes=64)
-            planes[(side, m)] = two.tile([P, L], U8, name="planes%d" % side, align_bytes=64)
-            nc.vector.quantize_mx(out=words[(side, m)][:].bitcast(FP8X4), scales=planes[(side, m)][:],
-                                  in_=grouped[(side, m)][:].rearrange("p r m c -> p (r m c)"))
+        def e_quantise(side, m, h):
+            if h == 0:
+                words[(side, m)] = three.tile([P, L], U32, name="words%d" % side, align_bytes=64)
+                planes[(side, m)] = three.tile([P, L], U8, name="planes%d" % side, align_bytes=64)
+            cols = slice(h * 2 * P, (h + 1) * 2 * P)
+            nc.vector.quantize_mx(out=words[(side, m)][:, cols].bitcast(FP8X4), scales=planes[(side, m)][:, cols],
+                                  in_=grouped[(side, m)][:, 2 * h:2 * h + 2].rearrange("p r m c -> p (r m c)"))
 
-        def products(m):
-            for side in range(2):
-                acc[(side, m)] = psum.tile([P, NB, D], F32, tag="o", name="acc")
-                other = (1 - side) * D
-                for q in range(NB):
-                    nc.tensor.matmul_mx(out=acc[(side, m)][:, q, :],
-                                        lhsT=words[(side, m)][:, q * P:(q + 1) * P].bitcast(FP8X4),
-                                        lhsT_scale=planes[(side, m)][:, q * P:(q + 1) * P],
-                                        rhs=xw[:, m, other:other + D].bitcast(FP8X4),
-                                        rhs_scale=xs[:, m, other:other + D],
-                                        start=True, stop=True)
-            nc.vector.reciprocal(out=ra[:, m, :], in_=suma[:, m, :])
-            nc.vector.reciprocal(out=rb[:, m, :], in_=sumb[:, m, :])
-            tmp[m] = two.tile([P, NB, D], F32, name="tmp")
-            osb[m] = three.tile([P, NB, D], F32, name="osb")
-
-        def finish(m, q):
-            nc.scalar.activation(out=tmp[m][:, q, :], in_=acc[(0, m)][:, q, :], func=ACT.Copy,
+        def scale_a(m, q):
+            lo = D if NMX == 2 * D else 0
+            tmp[(m, q)] = three.tile([P, D], F32, name="tmp")
+            nc.scalar.activation(out=tmp[(m, q)][:], in_=acc[(m, q)][:, 0, lo:lo + D], func=ACT.Copy,
                                  scale=ra[:, m, q:q + 1])
-            nc.vector.scalar_tensor_tensor(out=osb[m][:, q, :], in0=acc[(1, m)][:, q, :],
-                                           scalar=rb[:, m, q:q + 1], in1=tmp[m][:, q, :],
+
+        def scale_b_add(m, q):
+            if q == 0:
+                osb[m] = three.tile([P, NB, D], F32, name="osb")
+            nc.vector.scalar_tensor_tensor(out=osb[m][:, q, :], in0=acc[(m, q)][:, 1, 0:D],
+                                           scalar=rb[:, m, q:q + 1], in1=tmp[(m, q)][:],
                                            op0=ALU.mult, op1=ALU.add)
             if q == NB - 1:
                 nc.sync.dma_start(out=out[m].rearrange("(p q) d -> p q d", q=NB), in_=osb[m][:])
 
-        et_plan = [(0, 1, 0), (1, 2, 1), (0, 1, 1), (1, 1, 0)]
+        et_plan = [(0, 0, 4), (0, 1, 6), (1, 0, 7), (1, 1, 9)]
 
-        def quarter(k, q):
-            st_ps = None
-            if ok(k - 1):
-                st_ps = scores_t(k - 1, q)
-            if ok(k):
-                scores(k, q)
-            lag_m, lag_t = (k, q - 1) if q > 0 else (k - 1, NB - 1)
-            if ok(lag_m):
-                exp_a(lag_m, lag_t)
-            if ok(k - 1):
-                exp_b(k - 1, q, st_ps)
-            pk, pq = (k, q - 1) if q > 0 else (k - 1, NB - 1)
-            side, off, h = et_plan[pq]
-            if ok(pk - off):
-                e_regroup(side, pk - off, h)
-            side, off, h = et_plan[q]
-            if ok(k - off):
-                e_transposes(side, k - off, h)
-            if q == 0 and ok(k - 2):
-                e_quantise(0, k - 2)
-            if q == 1 and ok(k - 3):
-                products(k - 3)
-                finish(k - 3, 0)
-                finish(k - 3, 1)
-            if q == 2:
-                if ok(k - 3):
-                    finish(k - 3, 2)
-                    finish(k - 3, 3)
-                if ok(k + 1):
-                    x_transposes(k + 1)
-                    x_regroup(k + 1)
-            if q == 3:
-                if ok(k - 2):
-                    e_quantise(1, k - 2)
-                if ok(k + 1):
-                    x_quantise(k + 1)
+        def quarter(g):
+            st = split(g, 4)
+            st_ps = scores_t(st[0], st[1]) if st is not None else None
+            scores_and_products(split(g, 0), split(g, 12))
+            e = split(g, 1)
+            if e is not None:
+                exp_a(e[0], e[1])
+            if st is not None:
+                exp_b(st[0], st[1], st_ps)
+            for side, h, first in et_plan:
+                m = at(g, first + 1)
+                if m is not None:
+                    e_regroup(side, m, h)
+            for a in range(2):
+                m = at(g, 1 + 2 * a)
+                if m is not None:
+                    x_regroup(m, a)
+            for side, h, first in et_plan:
+                m = at(g, first)
+                if m is not None:
+                    e_transposes(side, m, h)
+            mx = split(g, 12)
+            if mx is not None:
+                scale_a(mx[0], mx[1])
+            for side, h, first in et_plan:
+                m = at(g, first + 3)
+                if m is not None:
+                    e_quantise(side, m, h)
+            mx = split(g, 13)
+            if mx is not None:
+                scale_b_add(mx[0], mx[1])
+            m = at(g, -2)
+            if m is not None:
+                x_transposes(m)
+            m = at(g, 5)
+            if m is not None:
+                x_quantise(m)
+            m = at(g, 11)
+            if m is not None:
+                nc.vector.reciprocal(out=ra[:, m, :], in_=suma[:, m, :])
+                nc.vector.reciprocal(out=rb[:, m, :], in_=sumb[:, m, :])
 
         if PIN:
             ctx.enter_context(tc.manual_schedule())
-        for k in range(-1, B + 4):
-            for q in range(NB):
-                quarter(k, q)
+        for g in range(-2, NB * (B - 1) + 17):
+            quarter(g)

@@ -17,8 +17,7 @@ P = 128
 NB = L // P
 SCALE = 1.0 / (D ** 0.5)
 FLOPS = 3 * 2 * B * L * L * D
-PIN = True
-NMX = 256
+PIN = False
 
 
 def tile_mutualcrossattention_t_kernel(tc, x1, x2, out):
@@ -49,15 +48,10 @@ def tile_mutualcrossattention_t_kernel(tc, x1, x2, out):
         ra = keep.tile([P, B, NB], F32, name="ra")
         rb = keep.tile([P, B, NB], F32, name="rb")
 
-        xT, xg, sn, ea, eb, half, grouped, words, planes, acc, tmp, osb = {}, {}, {}, {}, {}, {}, {}, {}, {}, {}, {}, {}
+        xT, xg, sn, ea, eb, grouped, words, planes, acc, tmp, osb = {}, {}, {}, {}, {}, {}, {}, {}, {}, {}, {}
 
-        def at(g, first):
-            m, r = divmod(g - first, NB)
-            return m if (r == 0 and 0 <= m < B) else None
-
-        def split(g, first):
-            m, q = divmod(g - first, NB)
-            return (m, q) if 0 <= m < B else None
+        def ok(m):
+            return 0 <= m < B
 
         def x_transposes(m):
             xt_ps = psum.tile([P, 2, NB, P], BF16, tag="s", name="xt_ps")
@@ -67,45 +61,23 @@ def tile_mutualcrossattention_t_kernel(tc, x1, x2, out):
             xT[m] = three.tile([P, 2, L], BF16, name="xT")
             nc.vector.tensor_copy(out=xT[m][:], in_=xt_ps[:].rearrange("p a t m -> p a (t m)"))
 
-        def x_regroup(m, a):
-            if a == 0:
-                xg[m] = two.tile([P, 2, D, NB], BF16, name="xg", align_bytes=64)
-            nc.gpsimd.tensor_scalar(out=xg[m][:, a], in0=xn[:, a, m].rearrange("p t d -> p d t"),
+        def x_regroup(m):
+            xg[m] = two.tile([P, 2, D, NB], BF16, name="xg", align_bytes=64)
+            nc.gpsimd.tensor_scalar(out=xg[m][:], in0=xn[:, :, m].rearrange("p a t d -> p a d t"),
                                     scalar1=1.0, scalar2=0.0, op0=ALU.mult, op1=ALU.add)
 
         def x_quantise(m):
             nc.vector.quantize_mx(out=xw[:, m, :].bitcast(FP8X4), scales=xs[:, m, :],
                                   in_=xg[m][:].rearrange("p a d t -> p (a d t)"))
 
-        def products(m, q):
-            acc[(m, q)] = psum.tile([P, 2, NMX], F32, tag="o", name="acc")
-            for side in range(2):
-                lo = 0 if NMX == 2 * D else (1 - side) * D
-                nc.tensor.matmul_mx(out=acc[(m, q)][:, side, :],
-                                    lhsT=words[(side, m)][:, q * P:(q + 1) * P].bitcast(FP8X4),
-                                    lhsT_scale=planes[(side, m)][:, q * P:(q + 1) * P],
-                                    rhs=xw[:, m, lo:lo + NMX].bitcast(FP8X4),
-                                    rhs_scale=xs[:, m, lo:lo + NMX],
-                                    start=True, stop=True)
-
-        def scores_and_products(sc, mx):
-            hw = L // 2
-            s_ps = None
-            if sc is not None:
-                m, t = sc
-                if t == 0:
-                    sn[m] = three.tile([P, NB, L], F32, name="sn")
-                s_ps = psum.tile([P, L], F32, tag="s", name="s_ps")
-                nc.tensor.matmul(out=s_ps[:, 0:hw], lhsT=xT[m][:, 0, t * P:(t + 1) * P], rhs=xT[m][:, 1, 0:hw],
-                                 start=True, stop=True)
-            if mx is not None:
-                products(mx[0], mx[1])
-            if sc is not None:
-                m, t = sc
-                nc.tensor.matmul(out=s_ps[:, hw:L], lhsT=xT[m][:, 0, t * P:(t + 1) * P], rhs=xT[m][:, 1, hw:L],
-                                 start=True, stop=True)
-                nc.vector.tensor_scalar(out=sn[m][:, t, :], in0=s_ps[:], scalar1=-SCALE, scalar2=None,
-                                        op0=ALU.mult, op1=ALU.min, accum_out=nma[:, m, t:t + 1])
+        def scores(m, t):
+            if t == 0:
+                sn[m] = three.tile([P, NB, L], F32, name="sn")
+            s_ps = psum.tile([P, L], F32, tag="s", name="s_ps")
+            nc.tensor.matmul(out=s_ps[:], lhsT=xT[m][:, 0, t * P:(t + 1) * P], rhs=xT[m][:, 1, :],
+                             start=True, stop=True)
+            nc.vector.tensor_scalar(out=sn[m][:, t, :], in0=s_ps[:], scalar1=-SCALE, scalar2=None,
+                                    op0=ALU.mult, op1=ALU.min, accum_out=nma[:, m, t:t + 1])
 
         def exp_a(m, t):
             if t == 0:
@@ -134,84 +106,82 @@ def tile_mutualcrossattention_t_kernel(tc, x1, x2, out):
                 for c in range(NB):
                     nc.tensor.transpose(out=et_ps[:, r, c, :], in_=src[:, 2 * h + r, c * P:(c + 1) * P],
                                         identity=ident_b[:])
-            half[(side, m, h)] = three.tile([P, 2, NB, P], BF16, name="half")
-            nc.scalar.copy(out=half[(side, m, h)][:], in_=et_ps[:])
-
-        def e_regroup(side, m, h):
             if h == 0:
                 grouped[(side, m)] = two.tile([P, NB, P, NB], BF16, name="grouped%d" % side, align_bytes=64)
-            nc.gpsimd.tensor_scalar(out=grouped[(side, m)][:, 2 * h:2 * h + 2],
-                                    in0=half[(side, m, h)][:].rearrange("p r c m -> p r m c"),
-                                    scalar1=1.0, scalar2=0.0, op0=ALU.mult, op1=ALU.add)
+            dst = grouped[(side, m)][:, 2 * h:2 * h + 2]
+            if side == 1 and h == 1:
+                nc.vector.tensor_copy(out=dst, in_=et_ps[:].rearrange("p r c m -> p r m c"))
+            else:
+                nc.scalar.copy(out=dst, in_=et_ps[:].rearrange("p r c m -> p r m c"))
 
-        def e_quantise(side, m, h):
-            if h == 0:
-                words[(side, m)] = three.tile([P, L], U32, name="words%d" % side, align_bytes=64)
-                planes[(side, m)] = three.tile([P, L], U8, name="planes%d" % side, align_bytes=64)
-            cols = slice(h * 2 * P, (h + 1) * 2 * P)
-            nc.vector.quantize_mx(out=words[(side, m)][:, cols].bitcast(FP8X4), scales=planes[(side, m)][:, cols],
-                                  in_=grouped[(side, m)][:, 2 * h:2 * h + 2].rearrange("p r m c -> p (r m c)"))
+        def e_quantise(side, m):
+            words[(side, m)] = two.tile([P, L], U32, name="words%d" % side, align_bytes=64)
+            planes[(side, m)] = two.tile([P, L], U8, name="planes%d" % side, align_bytes=64)
+            nc.vector.quantize_mx(out=words[(side, m)][:].bitcast(FP8X4), scales=planes[(side, m)][:],
+                                  in_=grouped[(side, m)][:].rearrange("p r m c -> p (r m c)"))
 
-        def scale_a(m, q):
-            lo = D if NMX == 2 * D else 0
-            tmp[(m, q)] = three.tile([P, D], F32, name="tmp")
-            nc.scalar.activation(out=tmp[(m, q)][:], in_=acc[(m, q)][:, 0, lo:lo + D], func=ACT.Copy,
+        def products(m):
+            for side in range(2):
+                acc[(side, m)] = psum.tile([P, NB, D], F32, tag="o", name="acc")
+                other = (1 - side) * D
+                for q in range(NB):
+                    nc.tensor.matmul_mx(out=acc[(side, m)][:, q, :],
+                                        lhsT=words[(side, m)][:, q * P:(q + 1) * P].bitcast(FP8X4),
+                                        lhsT_scale=planes[(side, m)][:, q * P:(q + 1) * P],
+                                        rhs=xw[:, m, other:other + D].bitcast(FP8X4),
+                                        rhs_scale=xs[:, m, other:other + D],
+                                        start=True, stop=True)
+            nc.vector.reciprocal(out=ra[:, m, :], in_=suma[:, m, :])
+            nc.vector.reciprocal(out=rb[:, m, :], in_=sumb[:, m, :])
+            tmp[m] = two.tile([P, NB, D], F32, name="tmp")
+            osb[m] = three.tile([P, NB, D], F32, name="osb")
+
+        def finish(m, q):
+            nc.scalar.activation(out=tmp[m][:, q, :], in_=acc[(0, m)][:, q, :], func=ACT.Copy,
                                  scale=ra[:, m, q:q + 1])
-
-        def scale_b_add(m, q):
-            if q == 0:
-                osb[m] = three.tile([P, NB, D], F32, name="osb")
-            nc.vector.scalar_tensor_tensor(out=osb[m][:, q, :], in0=acc[(m, q)][:, 1, 0:D],
-                                           scalar=rb[:, m, q:q + 1], in1=tmp[(m, q)][:],
+            nc.vector.scalar_tensor_tensor(out=osb[m][:, q, :], in0=acc[(1, m)][:, q, :],
+                                           scalar=rb[:, m, q:q + 1], in1=tmp[m][:, q, :],
                                            op0=ALU.mult, op1=ALU.add)
             if q == NB - 1:
                 nc.sync.dma_start(out=out[m].rearrange("(p q) d -> p q d", q=NB), in_=osb[m][:])
 
-        et_plan = [(0, 0, 4), (0, 1, 6), (1, 0, 7), (1, 1, 9)]
+        et_plan = [(0, 1, 0), (1, 2, 1), (0, 1, 1), (1, 1, 0)]
 
-        def quarter(g):
-            st = split(g, 4)
-            st_ps = scores_t(st[0], st[1]) if st is not None else None
-            scores_and_products(split(g, 0), split(g, 12))
-            e = split(g, 1)
-            if e is not None:
-                exp_a(e[0], e[1])
-            if st is not None:
-                exp_b(st[0], st[1], st_ps)
-            for side, h, first in et_plan:
-                m = at(g, first + 1)
-                if m is not None:
-                    e_regroup(side, m, h)
-            for a in range(2):
-                m = at(g, 1 + 2 * a)
-                if m is not None:
-                    x_regroup(m, a)
-            for side, h, first in et_plan:
-                m = at(g, first)
-                if m is not None:
-                    e_transposes(side, m, h)
-            mx = split(g, 12)
-            if mx is not None:
-                scale_a(mx[0], mx[1])
-            for side, h, first in et_plan:
-                m = at(g, first + 3)
-                if m is not None:
-                    e_quantise(side, m, h)
-            mx = split(g, 13)
-            if mx is not None:
-                scale_b_add(mx[0], mx[1])
-            m = at(g, -2)
-            if m is not None:
-                x_transposes(m)
-            m = at(g, 5)
-            if m is not None:
-                x_quantise(m)
-            m = at(g, 11)
-            if m is not None:
-                nc.vector.reciprocal(out=ra[:, m, :], in_=suma[:, m, :])
-                nc.vector.reciprocal(out=rb[:, m, :], in_=sumb[:, m, :])
+        def quarter(k, q):
+            st_ps = None
+            if ok(k - 1):
+                st_ps = scores_t(k - 1, q)
+            if ok(k):
+                scores(k, q)
+            lag_m, lag_t = (k, q - 1) if q > 0 else (k - 1, NB - 1)
+            if ok(lag_m):
+                exp_a(lag_m, lag_t)
+            if ok(k - 1):
+                exp_b(k - 1, q, st_ps)
+            side, off, h = et_plan[q]
+            if ok(k - off):
+                e_transposes(side, k - off, h)
+            if q == 0 and ok(k - 2):
+                e_quantise(0, k - 2)
+            if q == 1 and ok(k - 3):
+                products(k - 3)
+                finish(k - 3, 0)
+                finish(k - 3, 1)
+            if q == 2:
+                if ok(k - 3):
+                    finish(k - 3, 2)
+                    finish(k - 3, 3)
+                if ok(k + 1):
+                    x_transposes(k + 1)
+                    x_regroup(k + 1)
+            if q == 3:
+                if ok(k - 2):
+                    e_quantise(1, k - 2)
+                if ok(k + 1):
+                    x_quantise(k + 1)
 
         if PIN:
             ctx.enter_context(tc.manual_schedule())
-        for g in range(-2, NB * (B - 1) + 17):
-            quarter(g)
+        for k in range(-1, B + 4):
+            for q in range(NB):
+                quarter(k, q)

@@ -17,7 +17,8 @@ P = 128
 NB = L // P
 SCALE = 1.0 / (D ** 0.5)
 FLOPS = 3 * 2 * B * L * L * D
-PIN = False
+PIN = True
+NMX = 256
 
 
 def tile_mutualcrossattention_t_kernel(tc, x1, x2, out):
@@ -48,10 +49,15 @@ def tile_mutualcrossattention_t_kernel(tc, x1, x2, out):
         ra = keep.tile([P, B, NB], F32, name="ra")
         rb = keep.tile([P, B, NB], F32, name="rb")
 
-        xT, xg, sn, ea, eb, grouped, words, planes, acc, tmp, osb = {}, {}, {}, {}, {}, {}, {}, {}, {}, {}, {}
+        xT, xg, sn, ea, eb, half, grouped, words, planes, acc, tmp, osb = {}, {}, {}, {}, {}, {}, {}, {}, {}, {}, {}, {}
 
-        def ok(m):
-            return 0 <= m < B
+        def at(g, first):
+            m, r = divmod(g - first, NB)
+            return m if (r == 0 and 0 <= m < B) else None
+
+        def split(g, first):
+            m, q = divmod(g - first, NB)
+            return (m, q) if 0 <= m < B else None
 
         def x_transposes(m):
             xt_ps = psum.tile([P, 2, NB, P], BF16, tag="s", name="xt_ps")
@@ -59,25 +65,58 @@ def tile_mutualcrossattention_t_kernel(tc, x1, x2, out):
                 for t in range(NB):
                     nc.tensor.transpose(out=xt_ps[:, a, t, :], in_=xn[:, a, m, t, :], identity=ident_b[:])
             xT[m] = three.tile([P, 2, L], BF16, name="xT")
-            nc.vector.tensor_copy(out=xT[m][:], in_=xt_ps[:].rearrange("p a t m -> p a (t m)"))
+            nc.scalar.copy(out=xT[m][:], in_=xt_ps[:].rearrange("p a t m -> p a (t m)"))
 
-        def x_regroup(m):
-            xg[m] = two.tile([P, 2, D, NB], BF16, name="xg", align_bytes=64)
-            nc.gpsimd.tensor_scalar(out=xg[m][:], in0=xn[:, :, m].rearrange("p a t d -> p a d t"),
+        def x_regroup(m, a):
+            if a == 0:
+                xg[m] = two.tile([P, 2, D, NB], BF16, name="xg", align_bytes=64)
+            nc.gpsimd.tensor_scalar(out=xg[m][:, a], in0=xn[:, a, m].rearrange("p t d -> p d t"),
                                     scalar1=1.0, scalar2=0.0, op0=ALU.mult, op1=ALU.add)
 
         def x_quantise(m):
             nc.vector.quantize_mx(out=xw[:, m, :].bitcast(FP8X4), scales=xs[:, m, :],
                                   in_=xg[m][:].rearrange("p a d t -> p (a d t)"))
 
-        def scores(m, t):
-            if t == 0:
-                sn[m] = three.tile([P, NB, L], F32, name="sn")
-            s_ps = psum.tile([P, L], F32, tag="s", name="s_ps")
-            nc.tensor.matmul(out=s_ps[:], lhsT=xT[m][:, 0, t * P:(t + 1) * P], rhs=xT[m][:, 1, :],
-                             start=True, stop=True)
-            nc.vector.tensor_scalar(out=sn[m][:, t, :], in0=s_ps[:], scalar1=-SCALE, scalar2=None,
-                                    op0=ALU.mult, op1=ALU.min, accum_out=nma[:, m, t:t + 1])
+        def products(mx, warm):
+            if mx is None and not warm:
+                return
+            bank = psum.tile([P, 2, NMX], F32, tag="o", name="acc")
+            for i in range(1 if warm else 0):
+                nc.tensor.matmul_mx(out=bank[:].rearrange("p a n -> p (a n)"),
+                                    lhsT=xw[:, 0, 0:D].bitcast(FP8X4), lhsT_scale=xs[:, 0, 0:D],
+                                    rhs=xw[:, 0:2, :].rearrange("p b n -> p (b n)").bitcast(FP8X4),
+                                    rhs_scale=xs[:, 0:2, :].rearrange("p b n -> p (b n)"),
+                                    start=True, stop=True)
+            if mx is None:
+                return
+            m, q = mx
+            acc[(m, q)] = bank
+            for side in range(2):
+                lo = 0 if NMX == 2 * D else (1 - side) * D
+                nc.tensor.matmul_mx(out=acc[(m, q)][:, side, :],
+                                    lhsT=words[(side, m)][:, q * P:(q + 1) * P].bitcast(FP8X4),
+                                    lhsT_scale=planes[(side, m)][:, q * P:(q + 1) * P],
+                                    rhs=xw[:, m, lo:lo + NMX].bitcast(FP8X4),
+                                    rhs_scale=xs[:, m, lo:lo + NMX],
+                                    start=True, stop=True)
+
+        def scores_and_products(sc, mx, warm):
+            hw = L // 2
+            s_ps = None
+            if sc is not None:
+                m, t = sc
+                if t == 0:
+                    sn[m] = three.tile([P, NB, L], F32, name="sn")
+                s_ps = psum.tile([P, L], F32, tag="s", name="s_ps")
+                nc.tensor.matmul(out=s_ps[:, 0:hw], lhsT=xT[m][:, 0, t * P:(t + 1) * P], rhs=xT[m][:, 1, 0:hw],
+                                 start=True, stop=True)
+            products(mx, warm)
+            if sc is not None:
+                m, t = sc
+                nc.tensor.matmul(out=s_ps[:, hw:L], lhsT=xT[m][:, 0, t * P:(t + 1) * P], rhs=xT[m][:, 1, hw:L],
+                                 start=True, stop=True)
+                nc.vector.tensor_scalar(out=sn[m][:, t, :], in0=s_ps[:], scalar1=-SCALE, scalar2=None,
+                                        op0=ALU.mult, op1=ALU.min, accum_out=nma[:, m, t:t + 1])
 
         def exp_a(m, t):
             if t == 0:
@@ -106,82 +145,99 @@ def tile_mutualcrossattention_t_kernel(tc, x1, x2, out):
                 for c in range(NB):
                     nc.tensor.transpose(out=et_ps[:, r, c, :], in_=src[:, 2 * h + r, c * P:(c + 1) * P],
                                         identity=ident_b[:])
+            if side == 0:
+                half[(side, m, h)] = three.tile([P, 2, NB, P], BF16, name="half")
+                nc.scalar.copy(out=half[(side, m, h)][:], in_=et_ps[:])
+                return
             if h == 0:
                 grouped[(side, m)] = two.tile([P, NB, P, NB], BF16, name="grouped%d" % side, align_bytes=64)
             dst = grouped[(side, m)][:, 2 * h:2 * h + 2]
-            if side == 1 and h == 1:
-                nc.vector.tensor_copy(out=dst, in_=et_ps[:].rearrange("p r c m -> p r m c"))
-            else:
+            if h == 0:
                 nc.scalar.copy(out=dst, in_=et_ps[:].rearrange("p r c m -> p r m c"))
+            else:
+                nc.vector.tensor_copy(out=dst, in_=et_ps[:].rearrange("p r c m -> p r m c"))
 
-        def e_quantise(side, m):
-            words[(side, m)] = two.tile([P, L], U32, name="words%d" % side, align_bytes=64)
-            planes[(side, m)] = two.tile([P, L], U8, name="planes%d" % side, align_bytes=64)
-            nc.vector.quantize_mx(out=words[(side, m)][:].bitcast(FP8X4), scales=planes[(side, m)][:],
-                                  in_=grouped[(side, m)][:].rearrange("p r m c -> p (r m c)"))
+        def e_regroup(side, m, h):
+            if h == 0:
+                grouped[(side, m)] = two.tile([P, NB, P, NB], BF16, name="grouped%d" % side, align_bytes=64)
+            nc.gpsimd.tensor_scalar(out=grouped[(side, m)][:, 2 * h:2 * h + 2],
+                                    in0=half[(side, m, h)][:].rearrange("p r c m -> p r m c"),
+                                    scalar1=1.0, scalar2=0.0, op0=ALU.mult, op1=ALU.add)
 
-        def products(m):
-            for side in range(2):
-                acc[(side, m)] = psum.tile([P, NB, D], F32, tag="o", name="acc")
-                other = (1 - side) * D
-                for q in range(NB):
-                    nc.tensor.matmul_mx(out=acc[(side, m)][:, q, :],
-                                        lhsT=words[(side, m)][:, q * P:(q + 1) * P].bitcast(FP8X4),
-                                        lhsT_scale=planes[(side, m)][:, q * P:(q + 1) * P],
-                                        rhs=xw[:, m, other:other + D].bitcast(FP8X4),
-                                        rhs_scale=xs[:, m, other:other + D],
-                                        start=True, stop=True)
-            nc.vector.reciprocal(out=ra[:, m, :], in_=suma[:, m, :])
-            nc.vector.reciprocal(out=rb[:, m, :], in_=sumb[:, m, :])
-            tmp[m] = two.tile([P, NB, D], F32, name="tmp")
-            osb[m] = three.tile([P, NB, D], F32, name="osb")
+        def e_quantise(side, m, h):
+            if h == 0:
+                words[(side, m)] = three.tile([P, L], U32, name="words%d" % side, align_bytes=64)
+                planes[(side, m)] = three.tile([P, L], U8, name="planes%d" % side, align_bytes=64)
+            cols = slice(h * 2 * P, (h + 1) * 2 * P)
+            nc.vector.quantize_mx(out=words[(side, m)][:, cols].bitcast(FP8X4), scales=planes[(side, m)][:, cols],
+                                  in_=grouped[(side, m)][:, 2 * h:2 * h + 2].rearrange("p r m c -> p (r m c)"))
 
-        def finish(m, q):
-            nc.scalar.activation(out=tmp[m][:, q, :], in_=acc[(0, m)][:, q, :], func=ACT.Copy,
+        def scale_a(m, q):
+            lo = D if NMX == 2 * D else 0
+            tmp[(m, q)] = three.tile([P, D], F32, name="tmp")
+            nc.scalar.activation(out=tmp[(m, q)][:], in_=acc[(m, q)][:, 0, lo:lo + D], func=ACT.Copy,
                                  scale=ra[:, m, q:q + 1])
-            nc.vector.scalar_tensor_tensor(out=osb[m][:, q, :], in0=acc[(1, m)][:, q, :],
-                                           scalar=rb[:, m, q:q + 1], in1=tmp[m][:, q, :],
+
+        def scale_b_add(m, q):
+            if q == 0:
+                osb[m] = three.tile([P, NB, D], F32, name="osb")
+            nc.vector.scalar_tensor_tensor(out=osb[m][:, q, :], in0=acc[(m, q)][:, 1, 0:D],
+                                           scalar=rb[:, m, q:q + 1], in1=tmp[(m, q)][:],
                                            op0=ALU.mult, op1=ALU.add)
             if q == NB - 1:
                 nc.sync.dma_start(out=out[m].rearrange("(p q) d -> p q d", q=NB), in_=osb[m][:])
 
-        et_plan = [(0, 1, 0), (1, 2, 1), (0, 1, 1), (1, 1, 0)]
+        et_plan = [(0, 0, 4), (0, 1, 6), (1, 0, 7), (1, 1, 9)]
 
-        def quarter(k, q):
-            st_ps = None
-            if ok(k - 1):
-                st_ps = scores_t(k - 1, q)
-            if ok(k):
-                scores(k, q)
-            lag_m, lag_t = (k, q - 1) if q > 0 else (k - 1, NB - 1)
-            if ok(lag_m):
-                exp_a(lag_m, lag_t)
-            if ok(k - 1):
-                exp_b(k - 1, q, st_ps)
-            side, off, h = et_plan[q]
-            if ok(k - off):
-                e_transposes(side, k - off, h)
-            if q == 0 and ok(k - 2):
-                e_quantise(0, k - 2)
-            if q == 1 and ok(k - 3):
-                products(k - 3)
-                finish(k - 3, 0)
-                finish(k - 3, 1)
-            if q == 2:
-                if ok(k - 3):
-                    finish(k - 3, 2)
-                    finish(k - 3, 3)
-                if ok(k + 1):
-                    x_transposes(k + 1)
-                    x_regroup(k + 1)
-            if q == 3:
-                if ok(k - 2):
-                    e_quantise(1, k - 2)
-                if ok(k + 1):
-                    x_quantise(k + 1)
+        def quarter(g):
+            st = split(g, 4)
+            st_ps = scores_t(st[0], st[1]) if st is not None else None
+            if g >= 0:
+                scores_and_products(split(g, 0), split(g, 12), g >= 3)
+            e = split(g, 1)
+            if e is not None:
+                exp_a(e[0], e[1])
+            if st is not None:
+                exp_b(st[0], st[1], st_ps)
+            for side, h, first in et_plan:
+                m = at(g, first + 1)
+                if m is not None and side == 0:
+                    e_regroup(side, m, h)
+            for a in range(2):
+                m = at(g, 1 + 2 * a - 8)
+                if m is not None and m >= 2:
+                    x_regroup(m, a)
+            for side, h, first in et_plan:
+                m = at(g, first)
+                if m is not None:
+                    e_transposes(side, m, h)
+            mx = split(g, 12)
+            if mx is not None:
+                scale_a(mx[0], mx[1])
+            for side, h, first in et_plan:
+                m = at(g, first + 3)
+                if m is not None:
+                    e_quantise(side, m, h)
+            mx = split(g, 13)
+            if mx is not None:
+                scale_b_add(mx[0], mx[1])
+            m = at(g, -2)
+            if m is not None:
+                x_transposes(m)
+            m = at(g, 5 - 8)
+            if m is not None and m >= 2:
+                x_quantise(m)
+            if g in (-2, -1):
+                x_regroup(g + 2, 0)
+                x_regroup(g + 2, 1)
+            if g in (0, 1):
+                x_quantise(g)
+            m = at(g, 11)
+            if m is not None:
+                nc.vector.reciprocal(out=ra[:, m, :], in_=suma[:, m, :])
+                nc.vector.reciprocal(out=rb[:, m, :], in_=sumb[:, m, :])
 
         if PIN:
             ctx.enter_context(tc.manual_schedule())
-        for k in range(-1, B + 4):
-            for q in range(NB):
-                quarter(k, q)
+        for g in range(-2, NB * (B - 1) + 17):
+            quarter(g)

@@ -17,7 +17,6 @@ P = 128
 NB = L // P
 SCALE = 1.0 / (D ** 0.5)
 FLOPS = 3 * 2 * B * L * L * D
-PIN = True
 NMX = 256
 
 
@@ -49,7 +48,8 @@ def tile_mutualcrossattention_t_kernel(tc, x1, x2, out):
         ra = keep.tile([P, B, NB], F32, name="ra")
         rb = keep.tile([P, B, NB], F32, name="rb")
 
-        xT, xg, sn, ea, eb, half, grouped, words, planes, acc, tmp, osb = {}, {}, {}, {}, {}, {}, {}, {}, {}, {}, {}, {}
+        xT, xg, sn, stn, ee, half, grouped, words, planes, tmp, osb = {}, {}, {}, {}, {}, {}, {}, {}, {}, {}, {}
+        bank = {}
 
         def at(g, first):
             m, r = divmod(g - first, NB)
@@ -59,185 +59,170 @@ def tile_mutualcrossattention_t_kernel(tc, x1, x2, out):
             m, q = divmod(g - first, NB)
             return (m, q) if 0 <= m < B else None
 
-        def x_transposes(m):
-            xt_ps = psum.tile([P, 2, NB, P], BF16, tag="s", name="xt_ps")
-            for a in range(2):
+        ST_AT = 5
+        MX_AT = 14
+        plan = [(0, 0, 4, 5, 7, "S"), (0, 1, 6, 7, 9, "S"), (1, 0, 9, None, 12, "S"), (1, 1, 11, 12, 14, "V")]
+
+        def copy_out(engine, dst, src):
+            if engine == "S":
+                nc.scalar.copy(out=dst, in_=src)
+            else:
+                nc.vector.tensor_copy(out=dst, in_=src)
+
+        def tensor_engine(g):
+            st, sc, mx = split(g, ST_AT), split(g, 0), split(g, MX_AT)
+            if st is not None:
+                m, u = st
+                bank[("st", g)] = psum.tile([P, L], F32, tag="st", name="st_ps")
                 for t in range(NB):
-                    nc.tensor.transpose(out=xt_ps[:, a, t, :], in_=xn[:, a, m, t, :], identity=ident_b[:])
-            xT[m] = three.tile([P, 2, L], BF16, name="xT")
-            nc.scalar.copy(out=xT[m][:], in_=xt_ps[:].rearrange("p a t m -> p a (t m)"))
-
-        def x_regroup(m, a):
-            if a == 0:
-                xg[m] = two.tile([P, 2, D, NB], BF16, name="xg", align_bytes=64)
-            nc.gpsimd.tensor_scalar(out=xg[m][:, a], in0=xn[:, a, m].rearrange("p t d -> p d t"),
-                                    scalar1=1.0, scalar2=0.0, op0=ALU.mult, op1=ALU.add)
-
-        def x_quantise(m):
-            nc.vector.quantize_mx(out=xw[:, m, :].bitcast(FP8X4), scales=xs[:, m, :],
-                                  in_=xg[m][:].rearrange("p a d t -> p (a d t)"))
-
-        def products(mx, warm):
-            if mx is None and not warm:
-                return
-            bank = psum.tile([P, 2, NMX], F32, tag="o", name="acc")
-            for i in range(1 if warm else 0):
-                nc.tensor.matmul_mx(out=bank[:].rearrange("p a n -> p (a n)"),
-                                    lhsT=xw[:, 0, 0:D].bitcast(FP8X4), lhsT_scale=xs[:, 0, 0:D],
-                                    rhs=xw[:, 0:2, :].rearrange("p b n -> p (b n)").bitcast(FP8X4),
-                                    rhs_scale=xs[:, 0:2, :].rearrange("p b n -> p (b n)"),
-                                    start=True, stop=True)
-            if mx is None:
-                return
-            m, q = mx
-            acc[(m, q)] = bank
-            for side in range(2):
-                lo = 0 if NMX == 2 * D else (1 - side) * D
-                nc.tensor.matmul_mx(out=acc[(m, q)][:, side, :],
-                                    lhsT=words[(side, m)][:, q * P:(q + 1) * P].bitcast(FP8X4),
-                                    lhsT_scale=planes[(side, m)][:, q * P:(q + 1) * P],
-                                    rhs=xw[:, m, lo:lo + NMX].bitcast(FP8X4),
-                                    rhs_scale=xs[:, m, lo:lo + NMX],
-                                    start=True, stop=True)
-
-        def scores_and_products(sc, mx, warm):
+                    nc.tensor.transpose(out=bank[("st", g)][:, t * P:(t + 1) * P], in_=sn[m][:, t, u * P:(u + 1) * P],
+                                        identity=ident_f[:])
+            for side, h, et, rg, qz, eng in plan:
+                m = at(g, et)
+                if m is not None:
+                    bank[("et", g)] = psum.tile([P, 2, NB, P], BF16, tag="et", name="et_ps")
+                    for r in range(2):
+                        for c in range(NB):
+                            nc.tensor.transpose(out=bank[("et", g)][:, r, c, :],
+                                                in_=ee[(side, m)][:, 2 * h + r, c * P:(c + 1) * P], identity=ident_b[:])
             hw = L // 2
-            s_ps = None
+            if sc is not None:
+                m, t = sc
+                bank[("s", g)] = psum.tile([P, L], F32, tag="s", name="s_ps")
+                nc.tensor.matmul(out=bank[("s", g)][:, 0:hw], lhsT=xT[m][:, 0, t * P:(t + 1) * P],
+                                 rhs=xT[m][:, 1, 0:hw], start=True, stop=True)
+            if mx is not None:
+                m, q = mx
+                bank[("o", g)] = psum.tile([P, 2, NMX], F32, tag="o", name="acc")
+                for side in range(2):
+                    lo = 0 if NMX == 2 * D else (1 - side) * D
+                    nc.tensor.matmul_mx(out=bank[("o", g)][:, side, :],
+                                        lhsT=words[(side, m)][:, q * P:(q + 1) * P].bitcast(FP8X4),
+                                        lhsT_scale=planes[(side, m)][:, q * P:(q + 1) * P],
+                                        rhs=xw[:, m, lo:lo + NMX].bitcast(FP8X4),
+                                        rhs_scale=xs[:, m, lo:lo + NMX], start=True, stop=True)
+            if sc is not None:
+                m, t = sc
+                nc.tensor.matmul(out=bank[("s", g)][:, hw:L], lhsT=xT[m][:, 0, t * P:(t + 1) * P],
+                                 rhs=xT[m][:, 1, hw:L], start=True, stop=True)
+            m = at(g, -2)
+            if m is not None:
+                bank[("x", g)] = psum.tile([P, 2, NB, P], BF16, tag="s", name="xt_ps")
+                for a in range(2):
+                    for t in range(NB):
+                        nc.tensor.transpose(out=bank[("x", g)][:, a, t, :], in_=xn[:, a, m, t, :], identity=ident_b[:])
+
+        def copies_out(g):
+            for side, h, et, rg, qz, eng in plan:
+                m = at(g, et)
+                if m is None:
+                    continue
+                if rg is not None:
+                    half[(side, m, h)] = three.tile([P, 2, NB, P], BF16, name="half")
+                    copy_out(eng, half[(side, m, h)][:], bank[("et", g)][:])
+                else:
+                    if h == 0:
+                        grouped[(side, m)] = two.tile([P, NB, P, NB], BF16, name="grouped%d" % side, align_bytes=64)
+                    copy_out(eng, grouped[(side, m)][:, 2 * h:2 * h + 2],
+                             bank[("et", g)][:].rearrange("p r c m -> p r m c"))
+
+        def scale_a(g):
+            mx = split(g, MX_AT)
+            if mx is not None:
+                m, q = mx
+                lo = D if NMX == 2 * D else 0
+                tmp[(m, q)] = three.tile([P, D], F32, name="tmp")
+                nc.scalar.activation(out=tmp[(m, q)][:], in_=bank[("o", g)][:, 0, lo:lo + D], func=ACT.Copy,
+                                     scale=ra[:, m, q:q + 1])
+
+        def minima(g):
+            st, sc = split(g, ST_AT), split(g, 0)
+            if st is not None:
+                m, u = st
+                if u == 0:
+                    stn[m] = three.tile([P, NB, L], F32, name="stn")
+                nc.vector.tensor_scalar(out=stn[m][:, u, :], in0=bank[("st", g)][:], scalar1=1.0, scalar2=None,
+                                        op0=ALU.mult, op1=ALU.min, accum_out=nmb[:, m, u:u + 1])
             if sc is not None:
                 m, t = sc
                 if t == 0:
                     sn[m] = three.tile([P, NB, L], F32, name="sn")
-                s_ps = psum.tile([P, L], F32, tag="s", name="s_ps")
-                nc.tensor.matmul(out=s_ps[:, 0:hw], lhsT=xT[m][:, 0, t * P:(t + 1) * P], rhs=xT[m][:, 1, 0:hw],
-                                 start=True, stop=True)
-            products(mx, warm)
-            if sc is not None:
-                m, t = sc
-                nc.tensor.matmul(out=s_ps[:, hw:L], lhsT=xT[m][:, 0, t * P:(t + 1) * P], rhs=xT[m][:, 1, hw:L],
-                                 start=True, stop=True)
-                nc.vector.tensor_scalar(out=sn[m][:, t, :], in0=s_ps[:], scalar1=-SCALE, scalar2=None,
+                nc.vector.tensor_scalar(out=sn[m][:, t, :], in0=bank[("s", g)][:], scalar1=-SCALE, scalar2=None,
                                         op0=ALU.mult, op1=ALU.min, accum_out=nma[:, m, t:t + 1])
 
-        def exp_a(m, t):
-            if t == 0:
-                ea[m] = three.tile([P, NB, L], BF16, name="ea")
-            nc.scalar.activation(out=ea[m][:, t, :], in_=sn[m][:, t, :], func=ACT.Exp,
-                                 bias=nma[:, m, t:t + 1], scale=-1.0, accum_out=suma[:, m, t:t + 1])
+        def exps(g):
+            for side, first, src, low, total in ((0, 1, sn, nma, suma), (1, ST_AT + 1, stn, nmb, sumb)):
+                e = split(g, first)
+                if e is not None:
+                    m, t = e
+                    if t == 0:
+                        ee[(side, m)] = three.tile([P, NB, L], BF16, name="ee%d" % side)
+                    nc.scalar.activation(out=ee[(side, m)][:, t, :], in_=src[m][:, t, :], func=ACT.Exp,
+                                         bias=low[:, m, t:t + 1], scale=-1.0, accum_out=total[:, m, t:t + 1])
 
-        def scores_t(m, u):
-            st_ps = psum.tile([P, L], F32, tag="st", name="st_ps")
-            for t in range(NB):
-                nc.tensor.transpose(out=st_ps[:, t * P:(t + 1) * P], in_=sn[m][:, t, u * P:(u + 1) * P],
-                                    identity=ident_f[:])
-            nc.vector.tensor_reduce(out=nmb[:, m, u:u + 1], in_=st_ps[:], axis=AX.X, op=ALU.min)
-            return st_ps
-
-        def exp_b(m, u, st_ps):
-            if u == 0:
-                eb[m] = three.tile([P, NB, L], BF16, name="eb")
-            nc.scalar.activation(out=eb[m][:, u, :], in_=st_ps[:], func=ACT.Exp,
-                                 bias=nmb[:, m, u:u + 1], scale=-1.0, accum_out=sumb[:, m, u:u + 1])
-
-        def e_transposes(side, m, h):
-            src = ea[m] if side == 0 else eb[m]
-            et_ps = psum.tile([P, 2, NB, P], BF16, tag="et", name="et_ps")
-            for r in range(2):
-                for c in range(NB):
-                    nc.tensor.transpose(out=et_ps[:, r, c, :], in_=src[:, 2 * h + r, c * P:(c + 1) * P],
-                                        identity=ident_b[:])
-            if side == 0:
-                half[(side, m, h)] = three.tile([P, 2, NB, P], BF16, name="half")
-                nc.scalar.copy(out=half[(side, m, h)][:], in_=et_ps[:])
-                return
-            if h == 0:
-                grouped[(side, m)] = two.tile([P, NB, P, NB], BF16, name="grouped%d" % side, align_bytes=64)
-            dst = grouped[(side, m)][:, 2 * h:2 * h + 2]
-            if h == 0:
-                nc.scalar.copy(out=dst, in_=et_ps[:].rearrange("p r c m -> p r m c"))
-            else:
-                nc.vector.tensor_copy(out=dst, in_=et_ps[:].rearrange("p r c m -> p r m c"))
-
-        def e_regroup(side, m, h):
-            if h == 0:
-                grouped[(side, m)] = two.tile([P, NB, P, NB], BF16, name="grouped%d" % side, align_bytes=64)
-            nc.gpsimd.tensor_scalar(out=grouped[(side, m)][:, 2 * h:2 * h + 2],
-                                    in0=half[(side, m, h)][:].rearrange("p r c m -> p r m c"),
-                                    scalar1=1.0, scalar2=0.0, op0=ALU.mult, op1=ALU.add)
-
-        def e_quantise(side, m, h):
-            if h == 0:
-                words[(side, m)] = three.tile([P, L], U32, name="words%d" % side, align_bytes=64)
-                planes[(side, m)] = three.tile([P, L], U8, name="planes%d" % side, align_bytes=64)
-            cols = slice(h * 2 * P, (h + 1) * 2 * P)
-            nc.vector.quantize_mx(out=words[(side, m)][:, cols].bitcast(FP8X4), scales=planes[(side, m)][:, cols],
-                                  in_=grouped[(side, m)][:, 2 * h:2 * h + 2].rearrange("p r m c -> p (r m c)"))
-
-        def scale_a(m, q):
-            lo = D if NMX == 2 * D else 0
-            tmp[(m, q)] = three.tile([P, D], F32, name="tmp")
-            nc.scalar.activation(out=tmp[(m, q)][:], in_=acc[(m, q)][:, 0, lo:lo + D], func=ACT.Copy,
-                                 scale=ra[:, m, q:q + 1])
-
-        def scale_b_add(m, q):
-            if q == 0:
-                osb[m] = three.tile([P, NB, D], F32, name="osb")
-            nc.vector.scalar_tensor_tensor(out=osb[m][:, q, :], in0=acc[(m, q)][:, 1, 0:D],
-                                           scalar=rb[:, m, q:q + 1], in1=tmp[(m, q)][:],
-                                           op0=ALU.mult, op1=ALU.add)
-            if q == NB - 1:
-                nc.sync.dma_start(out=out[m].rearrange("(p q) d -> p q d", q=NB), in_=osb[m][:])
-
-        et_plan = [(0, 0, 4), (0, 1, 6), (1, 0, 7), (1, 1, 9)]
-
-        def quarter(g):
-            st = split(g, 4)
-            st_ps = scores_t(st[0], st[1]) if st is not None else None
-            if g >= 0:
-                scores_and_products(split(g, 0), split(g, 12), g >= 3)
-            e = split(g, 1)
-            if e is not None:
-                exp_a(e[0], e[1])
-            if st is not None:
-                exp_b(st[0], st[1], st_ps)
-            for side, h, first in et_plan:
-                m = at(g, first + 1)
-                if m is not None and side == 0:
-                    e_regroup(side, m, h)
+        def gpsimd(g):
+            for side, h, et, rg, qz, eng in plan:
+                m = at(g, rg) if rg is not None else None
+                if m is not None:
+                    if h == 0:
+                        grouped[(side, m)] = two.tile([P, NB, P, NB], BF16, name="grouped%d" % side, align_bytes=64)
+                    nc.gpsimd.tensor_scalar(out=grouped[(side, m)][:, 2 * h:2 * h + 2],
+                                            in0=half[(side, m, h)][:].rearrange("p r c m -> p r m c"),
+                                            scalar1=1.0, scalar2=0.0, op0=ALU.mult, op1=ALU.add)
             for a in range(2):
-                m = at(g, 1 + 2 * a - 8)
-                if m is not None and m >= 2:
-                    x_regroup(m, a)
-            for side, h, first in et_plan:
-                m = at(g, first)
+                m = at(g, 1 + 2 * a)
                 if m is not None:
-                    e_transposes(side, m, h)
-            mx = split(g, 12)
-            if mx is not None:
-                scale_a(mx[0], mx[1])
-            for side, h, first in et_plan:
-                m = at(g, first + 3)
+                    if a == 0:
+                        xg[m] = two.tile([P, 2, D, NB], BF16, name="xg", align_bytes=64)
+                    nc.gpsimd.tensor_scalar(out=xg[m][:, a], in0=xn[:, a, m].rearrange("p t d -> p d t"),
+                                            scalar1=1.0, scalar2=0.0, op0=ALU.mult, op1=ALU.add)
+
+        def quantises(g):
+            for side, h, et, rg, qz, eng in plan:
+                m = at(g, qz)
                 if m is not None:
-                    e_quantise(side, m, h)
-            mx = split(g, 13)
+                    if h == 0:
+                        words[(side, m)] = three.tile([P, L], U32, name="words%d" % side, align_bytes=64)
+                        planes[(side, m)] = three.tile([P, L], U8, name="planes%d" % side, align_bytes=64)
+                    cols = slice(h * 2 * P, (h + 1) * 2 * P)
+                    nc.vector.quantize_mx(out=words[(side, m)][:, cols].bitcast(FP8X4),
+                                          scales=planes[(side, m)][:, cols],
+                                          in_=grouped[(side, m)][:, 2 * h:2 * h + 2].rearrange("p r m c -> p (r m c)"))
+
+        def scale_b_add(g):
+            mx = split(g, MX_AT)
             if mx is not None:
-                scale_b_add(mx[0], mx[1])
+                m, q = mx
+                if q == 0:
+                    osb[m] = three.tile([P, NB, D], F32, name="osb")
+                nc.vector.scalar_tensor_tensor(out=osb[m][:, q, :], in0=bank[("o", g)][:, 1, 0:D],
+                                               scalar=rb[:, m, q:q + 1], in1=tmp[(m, q)][:],
+                                               op0=ALU.mult, op1=ALU.add)
+                if q == NB - 1:
+                    nc.sync.dma_start(out=out[m].rearrange("(p q) d -> p q d", q=NB), in_=osb[m][:])
+
+        def rest(g):
             m = at(g, -2)
             if m is not None:
-                x_transposes(m)
-            m = at(g, 5 - 8)
-            if m is not None and m >= 2:
-                x_quantise(m)
-            if g in (-2, -1):
-                x_regroup(g + 2, 0)
-                x_regroup(g + 2, 1)
-            if g in (0, 1):
-                x_quantise(g)
-            m = at(g, 11)
+                xT[m] = three.tile([P, 2, L], BF16, name="xT")
+                nc.scalar.copy(out=xT[m][:], in_=bank[("x", g)][:].rearrange("p a t m -> p a (t m)"))
+            m = at(g, 5)
+            if m is not None:
+                nc.vector.quantize_mx(out=xw[:, m, :].bitcast(FP8X4), scales=xs[:, m, :],
+                                      in_=xg[m][:].rearrange("p a d t -> p (a d t)"))
+            m = at(g, MX_AT - 1)
             if m is not None:
                 nc.vector.reciprocal(out=ra[:, m, :], in_=suma[:, m, :])
                 nc.vector.reciprocal(out=rb[:, m, :], in_=sumb[:, m, :])
 
-        if PIN:
-            ctx.enter_context(tc.manual_schedule())
-        for g in range(-2, NB * (B - 1) + 17):
-            quarter(g)
+        ctx.enter_context(tc.manual_schedule())
+        for g in range(-2, NB * (B - 1) + MX_AT + NB):
+            tensor_engine(g)
+            copies_out(g)
+            scale_a(g)
+            minima(g)
+            exps(g)
+            gpsimd(g)
+            quantises(g)
+            scale_b_add(g)
+            rest(g)

@@ -43,10 +43,8 @@ def tile_mutualcrossattention_t_kernel(tc, x1, x2, out):
         xs = keep.tile([P, B, 2 * D], U8, name="xs", align_bytes=64)
         nma = keep.tile([P, B, NB], F32, name="nma")
         nmb = keep.tile([P, B, NB], F32, name="nmb")
-        suma = keep.tile([P, B, NB], F32, name="suma")
-        sumb = keep.tile([P, B, NB], F32, name="sumb")
-        ra = keep.tile([P, B, NB], F32, name="ra")
-        rb = keep.tile([P, B, NB], F32, name="rb")
+        sums = keep.tile([P, B, 2, NB], F32, name="sums")
+        rcp = keep.tile([P, B, 2, NB], F32, name="rcp")
 
         xT, xg, sn, stn, ee, half, grouped, words, planes, tmp, osb = {}, {}, {}, {}, {}, {}, {}, {}, {}, {}, {}
         bank = {}
@@ -60,8 +58,8 @@ def tile_mutualcrossattention_t_kernel(tc, x1, x2, out):
             return (m, q) if 0 <= m < B else None
 
         ST_AT = 5
-        MX_AT = 14
-        plan = [(0, 0, 4, 5, 7, "S"), (0, 1, 6, 7, 9, "S"), (1, 0, 9, None, 12, "S"), (1, 1, 11, 12, 14, "V")]
+        MX_AT = 15
+        plan = [(0, 0, 4, 5, 10, "S"), (0, 1, 6, 7, 10, "S"), (1, 0, 9, None, 14, "S"), (1, 1, 11, 12, 14, "V")]
 
         def copy_out(engine, dst, src):
             if engine == "S":
@@ -133,7 +131,7 @@ def tile_mutualcrossattention_t_kernel(tc, x1, x2, out):
                 lo = D if NMX == 2 * D else 0
                 tmp[(m, q)] = three.tile([P, D], F32, name="tmp")
                 nc.scalar.activation(out=tmp[(m, q)][:], in_=bank[("o", g)][:, 0, lo:lo + D], func=ACT.Copy,
-                                     scale=ra[:, m, q:q + 1])
+                                     scale=rcp[:, m, 0, q:q + 1])
 
         def minima(g):
             st, sc = split(g, ST_AT), split(g, 0)
@@ -151,14 +149,14 @@ def tile_mutualcrossattention_t_kernel(tc, x1, x2, out):
                                         op0=ALU.mult, op1=ALU.min, accum_out=nma[:, m, t:t + 1])
 
         def exps(g):
-            for side, first, src, low, total in ((0, 1, sn, nma, suma), (1, ST_AT + 1, stn, nmb, sumb)):
+            for side, first, src, low in ((0, 1, sn, nma), (1, ST_AT + 1, stn, nmb)):
                 e = split(g, first)
                 if e is not None:
                     m, t = e
                     if t == 0:
                         ee[(side, m)] = three.tile([P, NB, L], BF16, name="ee%d" % side)
                     nc.scalar.activation(out=ee[(side, m)][:, t, :], in_=src[m][:, t, :], func=ACT.Exp,
-                                         bias=low[:, m, t:t + 1], scale=-1.0, accum_out=total[:, m, t:t + 1])
+                                         bias=low[:, m, t:t + 1], scale=-1.0, accum_out=sums[:, m, side, t:t + 1])
 
         def gpsimd(g):
             for side, h, et, rg, qz, eng in plan:
@@ -169,25 +167,24 @@ def tile_mutualcrossattention_t_kernel(tc, x1, x2, out):
                     nc.gpsimd.tensor_scalar(out=grouped[(side, m)][:, 2 * h:2 * h + 2],
                                             in0=half[(side, m, h)][:].rearrange("p r c m -> p r m c"),
                                             scalar1=1.0, scalar2=0.0, op0=ALU.mult, op1=ALU.add)
-            for a in range(2):
-                m = at(g, 1 + 2 * a)
-                if m is not None:
-                    if a == 0:
-                        xg[m] = two.tile([P, 2, D, NB], BF16, name="xg", align_bytes=64)
-                    nc.gpsimd.tensor_scalar(out=xg[m][:, a], in0=xn[:, a, m].rearrange("p t d -> p d t"),
-                                            scalar1=1.0, scalar2=0.0, op0=ALU.mult, op1=ALU.add)
+            m = at(g, 1)
+            if m is not None:
+                xg[m] = two.tile([P, 2, D, NB], BF16, name="xg", align_bytes=64)
+                nc.gpsimd.tensor_scalar(out=xg[m][:], in0=xn[:, :, m].rearrange("p a t d -> p a d t"),
+                                        scalar1=1.0, scalar2=0.0, op0=ALU.mult, op1=ALU.add)
 
         def quantises(g):
             for side, h, et, rg, qz, eng in plan:
                 m = at(g, qz)
-                if m is not None:
-                    if h == 0:
-                        words[(side, m)] = three.tile([P, L], U32, name="words%d" % side, align_bytes=64)
-                        planes[(side, m)] = three.tile([P, L], U8, name="planes%d" % side, align_bytes=64)
-                    cols = slice(h * 2 * P, (h + 1) * 2 * P)
-                    nc.vector.quantize_mx(out=words[(side, m)][:, cols].bitcast(FP8X4),
-                                          scales=planes[(side, m)][:, cols],
-                                          in_=grouped[(side, m)][:, 2 * h:2 * h + 2].rearrange("p r m c -> p (r m c)"))
+                if m is not None and h == 1:
+                    words[(side, m)] = three.tile([P, L], U32, name="words%d" % side, align_bytes=64)
+                    planes[(side, m)] = three.tile([P, L], U8, name="planes%d" % side, align_bytes=64)
+                    nc.vector.quantize_mx(out=words[(side, m)][:].bitcast(FP8X4), scales=planes[(side, m)][:],
+                                          in_=grouped[(side, m)][:].rearrange("p r m c -> p (r m c)"))
+            m = at(g, 6)
+            if m is not None:
+                nc.vector.quantize_mx(out=xw[:, m, :].bitcast(FP8X4), scales=xs[:, m, :],
+                                      in_=xg[m][:].rearrange("p a d t -> p (a d t)"))
 
         def scale_b_add(g):
             mx = split(g, MX_AT)
@@ -196,7 +193,7 @@ def tile_mutualcrossattention_t_kernel(tc, x1, x2, out):
                 if q == 0:
                     osb[m] = three.tile([P, NB, D], F32, name="osb")
                 nc.vector.scalar_tensor_tensor(out=osb[m][:, q, :], in0=bank[("o", g)][:, 1, 0:D],
-                                               scalar=rb[:, m, q:q + 1], in1=tmp[(m, q)][:],
+                                               scalar=rcp[:, m, 1, q:q + 1], in1=tmp[(m, q)][:],
                                                op0=ALU.mult, op1=ALU.add)
                 if q == NB - 1:
                     nc.sync.dma_start(out=out[m].rearrange("(p q) d -> p q d", q=NB), in_=osb[m][:])
@@ -206,14 +203,9 @@ def tile_mutualcrossattention_t_kernel(tc, x1, x2, out):
             if m is not None:
                 xT[m] = three.tile([P, 2, L], BF16, name="xT")
                 nc.scalar.copy(out=xT[m][:], in_=bank[("x", g)][:].rearrange("p a t m -> p a (t m)"))
-            m = at(g, 5)
-            if m is not None:
-                nc.vector.quantize_mx(out=xw[:, m, :].bitcast(FP8X4), scales=xs[:, m, :],
-                                      in_=xg[m][:].rearrange("p a d t -> p (a d t)"))
             m = at(g, MX_AT - 1)
             if m is not None:
-                nc.vector.reciprocal(out=ra[:, m, :], in_=suma[:, m, :])
-                nc.vector.reciprocal(out=rb[:, m, :], in_=sumb[:, m, :])
+                nc.vector.reciprocal(out=rcp[:, m], in_=sums[:, m])
 
         ctx.enter_context(tc.manual_schedule())
         for g in range(-2, NB * (B - 1) + MX_AT + NB):

@@ -58,8 +58,8 @@ def tile_mutualcrossattention_t_kernel(tc, x1, x2, out):
             return (m, q) if 0 <= m < B else None
 
         ST_AT = 5
-        MX_AT = 15
-        plan = [(0, 0, 4, 5, 10, "S"), (0, 1, 6, 7, 10, "S"), (1, 0, 9, None, 14, "S"), (1, 1, 11, 12, 14, "V")]
+        MX_AT = 16
+        plan = [(0, 0, 4, 5, 11, "S"), (0, 1, 6, 7, 11, "S"), (1, 0, 9, None, 15, "S"), (1, 1, 11, 12, 15, "V")]
 
         def copy_out(engine, dst, src):
             if engine == "S":
@@ -110,10 +110,10 @@ def tile_mutualcrossattention_t_kernel(tc, x1, x2, out):
                     for t in range(NB):
                         nc.tensor.transpose(out=bank[("x", g)][:, a, t, :], in_=xn[:, a, m, t, :], identity=ident_b[:])
 
-        def copies_out(g):
+        def copies_out(g, engine):
             for side, h, et, rg, qz, eng in plan:
                 m = at(g, et)
-                if m is None:
+                if m is None or eng != engine:
                     continue
                 if rg is not None:
                     half[(side, m, h)] = three.tile([P, 2, NB, P], BF16, name="half")
@@ -181,7 +181,7 @@ def tile_mutualcrossattention_t_kernel(tc, x1, x2, out):
                     planes[(side, m)] = three.tile([P, L], U8, name="planes%d" % side, align_bytes=64)
                     nc.vector.quantize_mx(out=words[(side, m)][:].bitcast(FP8X4), scales=planes[(side, m)][:],
                                           in_=grouped[(side, m)][:].rearrange("p r m c -> p (r m c)"))
-            m = at(g, 6)
+            m = at(g, 7)
             if m is not None:
                 nc.vector.quantize_mx(out=xw[:, m, :].bitcast(FP8X4), scales=xs[:, m, :],
                                       in_=xg[m][:].rearrange("p a d t -> p (a d t)"))
@@ -210,11 +210,12 @@ def tile_mutualcrossattention_t_kernel(tc, x1, x2, out):
         ctx.enter_context(tc.manual_schedule())
         for g in range(-2, NB * (B - 1) + MX_AT + NB):
             tensor_engine(g)
-            copies_out(g)
+            copies_out(g, "S")
             scale_a(g)
             minima(g)
             exps(g)
             gpsimd(g)
             quantises(g)
+            copies_out(g, "V")
             scale_b_add(g)
             rest(g)

@@ -58,8 +58,8 @@ def tile_mutualcrossattention_t_kernel(tc, x1, x2, out):
             return (m, q) if 0 <= m < B else None
 
         ST_AT = 5
-        MX_AT = 16
-        plan = [(0, 0, 4, 5, 11, "S"), (0, 1, 6, 7, 11, "S"), (1, 0, 9, None, 15, "S"), (1, 1, 11, 12, 15, "V")]
+        MX_AT = 14
+        plan = [(0, 0, 4, 5, 9, "S"), (0, 1, 6, 7, 9, "S"), (1, 0, 9, None, 13, "S"), (1, 1, 11, 12, 13, "V")]
 
         def copy_out(engine, dst, src):
             if engine == "S":
@@ -103,17 +103,17 @@ def tile_mutualcrossattention_t_kernel(tc, x1, x2, out):
                 m, t = sc
                 nc.tensor.matmul(out=bank[("s", g)][:, hw:L], lhsT=xT[m][:, 0, t * P:(t + 1) * P],
                                  rhs=xT[m][:, 1, hw:L], start=True, stop=True)
-            m = at(g, -2)
+            m = at(g, -5)
             if m is not None:
                 bank[("x", g)] = psum.tile([P, 2, NB, P], BF16, tag="s", name="xt_ps")
                 for a in range(2):
                     for t in range(NB):
                         nc.tensor.transpose(out=bank[("x", g)][:, a, t, :], in_=xn[:, a, m, t, :], identity=ident_b[:])
 
-        def copies_out(g, engine):
+        def copies_out(g):
             for side, h, et, rg, qz, eng in plan:
                 m = at(g, et)
-                if m is None or eng != engine:
+                if m is None:
                     continue
                 if rg is not None:
                     half[(side, m, h)] = three.tile([P, 2, NB, P], BF16, name="half")
@@ -167,7 +167,7 @@ def tile_mutualcrossattention_t_kernel(tc, x1, x2, out):
                     nc.gpsimd.tensor_scalar(out=grouped[(side, m)][:, 2 * h:2 * h + 2],
                                             in0=half[(side, m, h)][:].rearrange("p r c m -> p r m c"),
                                             scalar1=1.0, scalar2=0.0, op0=ALU.mult, op1=ALU.add)
-            m = at(g, 1)
+            m = at(g, 3)
             if m is not None:
                 xg[m] = two.tile([P, 2, D, NB], BF16, name="xg", align_bytes=64)
                 nc.gpsimd.tensor_scalar(out=xg[m][:], in0=xn[:, :, m].rearrange("p a t d -> p a d t"),
@@ -181,7 +181,7 @@ def tile_mutualcrossattention_t_kernel(tc, x1, x2, out):
                     planes[(side, m)] = three.tile([P, L], U8, name="planes%d" % side, align_bytes=64)
                     nc.vector.quantize_mx(out=words[(side, m)][:].bitcast(FP8X4), scales=planes[(side, m)][:],
                                           in_=grouped[(side, m)][:].rearrange("p r m c -> p (r m c)"))
-            m = at(g, 7)
+            m = at(g, 5)
             if m is not None:
                 nc.vector.quantize_mx(out=xw[:, m, :].bitcast(FP8X4), scales=xs[:, m, :],
                                       in_=xg[m][:].rearrange("p a d t -> p (a d t)"))
@@ -199,7 +199,7 @@ def tile_mutualcrossattention_t_kernel(tc, x1, x2, out):
                     nc.sync.dma_start(out=out[m].rearrange("(p q) d -> p q d", q=NB), in_=osb[m][:])
 
         def rest(g):
-            m = at(g, -2)
+            m = at(g, -5)
             if m is not None:
                 xT[m] = three.tile([P, 2, L], BF16, name="xT")
                 nc.scalar.copy(out=xT[m][:], in_=bank[("x", g)][:].rearrange("p a t m -> p a (t m)"))
@@ -208,14 +208,13 @@ def tile_mutualcrossattention_t_kernel(tc, x1, x2, out):
                 nc.vector.reciprocal(out=rcp[:, m], in_=sums[:, m])
 
         ctx.enter_context(tc.manual_schedule())
-        for g in range(-2, NB * (B - 1) + MX_AT + NB):
+        for g in range(-5, NB * (B - 1) + MX_AT + NB):
             tensor_engine(g)
-            copies_out(g, "S")
+            copies_out(g)
             scale_a(g)
             minima(g)
             exps(g)
             gpsimd(g)
             quantises(g)
-            copies_out(g, "V")
             scale_b_add(g)
             rest(g)

@@ -46,7 +46,7 @@ def tile_mutualcrossattention_t_kernel(tc, x1, x2, out):
         sums = keep.tile([P, B, 2, NB], F32, name="sums")
         rcp = keep.tile([P, B, 2, NB], F32, name="rcp")
 
-        xT, xg, sn, stn, ee, half, grouped, words, planes, tmp, osb = {}, {}, {}, {}, {}, {}, {}, {}, {}, {}, {}
+        xT, xg, sn, stn, ee, grouped, words, planes, tmp, osb = {}, {}, {}, {}, {}, {}, {}, {}, {}, {}
         bank = {}
 
         def at(g, first):
@@ -59,7 +59,8 @@ def tile_mutualcrossattention_t_kernel(tc, x1, x2, out):
 
         ST_AT = 5
         MX_AT = 14
-        plan = [(0, 0, 4, 5, 9, "S"), (0, 1, 6, 7, 9, "S"), (1, 0, 9, None, 13, "S"), (1, 1, 11, 12, 13, "V")]
+        XQ_AT = 6
+        plan = [(0, 0, 4, 8, "S"), (0, 1, 6, 8, "S"), (1, 0, 9, 13, "S"), (1, 1, 11, 13, "V")]
 
         def copy_out(engine, dst, src):
             if engine == "S":
@@ -75,14 +76,15 @@ def tile_mutualcrossattention_t_kernel(tc, x1, x2, out):
                 for t in range(NB):
                     nc.tensor.transpose(out=bank[("st", g)][:, t * P:(t + 1) * P], in_=sn[m][:, t, u * P:(u + 1) * P],
                                         identity=ident_f[:])
-            for side, h, et, rg, qz, eng in plan:
+            for side, h, et, qz, eng in plan:
                 m = at(g, et)
                 if m is not None:
-                    bank[("et", g)] = psum.tile([P, 2, NB, P], BF16, tag="et", name="et_ps")
+                    bank[("et", g)] = psum.tile([P, 2, 2, P], F32, tag="et", name="et_ps")
                     for r in range(2):
-                        for c in range(NB):
-                            nc.tensor.transpose(out=bank[("et", g)][:, r, c, :],
-                                                in_=ee[(side, m)][:, 2 * h + r, c * P:(c + 1) * P], identity=ident_b[:])
+                        pairs = ee[(side, m)][:, 2 * h + r, :].bitcast(F32)
+                        for u in range(2):
+                            nc.tensor.transpose(out=bank[("et", g)][:, r, u, :], in_=pairs[:, u * P:(u + 1) * P],
+                                                identity=ident_f[:])
             hw = L // 2
             if sc is not None:
                 m, t = sc
@@ -111,18 +113,14 @@ def tile_mutualcrossattention_t_kernel(tc, x1, x2, out):
                         nc.tensor.transpose(out=bank[("x", g)][:, a, t, :], in_=xn[:, a, m, t, :], identity=ident_b[:])
 
         def copies_out(g):
-            for side, h, et, rg, qz, eng in plan:
+            for side, h, et, qz, eng in plan:
                 m = at(g, et)
                 if m is None:
                     continue
-                if rg is not None:
-                    half[(side, m, h)] = three.tile([P, 2, NB, P], BF16, name="half")
-                    copy_out(eng, half[(side, m, h)][:], bank[("et", g)][:])
-                else:
-                    if h == 0:
-                        grouped[(side, m)] = two.tile([P, NB, P, NB], BF16, name="grouped%d" % side, align_bytes=64)
-                    copy_out(eng, grouped[(side, m)][:, 2 * h:2 * h + 2],
-                             bank[("et", g)][:].rearrange("p r c m -> p r m c"))
+                if h == 0:
+                    grouped[(side, m)] = two.tile([P, NB, P, NB], BF16, name="grouped%d" % side, align_bytes=64)
+                copy_out(eng, grouped[(side, m)][:, 2 * h:2 * h + 2].bitcast(F32),
+                         bank[("et", g)][:].rearrange("p r u m -> p r m u"))
 
         def scale_a(g):
             mx = split(g, MX_AT)
@@ -155,18 +153,11 @@ def tile_mutualcrossattention_t_kernel(tc, x1, x2, out):
                     m, t = e
                     if t == 0:
                         ee[(side, m)] = three.tile([P, NB, L], BF16, name="ee%d" % side)
-                    nc.scalar.activation(out=ee[(side, m)][:, t, :], in_=src[m][:, t, :], func=ACT.Exp,
+                    nc.scalar.activation(out=ee[(side, m)][:, t, :].rearrange("p (u q e) -> p u q e", u=2, e=2),
+                                         in_=src[m][:, t, :].rearrange("p (u e q) -> p u q e", u=2, e=2), func=ACT.Exp,
                                          bias=low[:, m, t:t + 1], scale=-1.0, accum_out=sums[:, m, side, t:t + 1])
 
         def gpsimd(g):
-            for side, h, et, rg, qz, eng in plan:
-                m = at(g, rg) if rg is not None else None
-                if m is not None:
-                    if h == 0:
-                        grouped[(side, m)] = two.tile([P, NB, P, NB], BF16, name="grouped%d" % side, align_bytes=64)
-                    nc.gpsimd.tensor_scalar(out=grouped[(side, m)][:, 2 * h:2 * h + 2],
-                                            in0=half[(side, m, h)][:].rearrange("p r c m -> p r m c"),
-                                            scalar1=1.0, scalar2=0.0, op0=ALU.mult, op1=ALU.add)
             m = at(g, 3)
             if m is not None:
                 xg[m] = two.tile([P, 2, D, NB], BF16, name="xg", align_bytes=64)
@@ -174,14 +165,14 @@ def tile_mutualcrossattention_t_kernel(tc, x1, x2, out):
                                         scalar1=1.0, scalar2=0.0, op0=ALU.mult, op1=ALU.add)
 
         def quantises(g):
-            for side, h, et, rg, qz, eng in plan:
+            for side, h, et, qz, eng in plan:
                 m = at(g, qz)
                 if m is not None and h == 1:
                     words[(side, m)] = three.tile([P, L], U32, name="words%d" % side, align_bytes=64)
                     planes[(side, m)] = three.tile([P, L], U8, name="planes%d" % side, align_bytes=64)
                     nc.vector.quantize_mx(out=words[(side, m)][:].bitcast(FP8X4), scales=planes[(side, m)][:],
                                           in_=grouped[(side, m)][:].rearrange("p r m c -> p (r m c)"))
-            m = at(g, 5)
+            m = at(g, XQ_AT)
             if m is not None:
                 nc.vector.quantize_mx(out=xw[:, m, :].bitcast(FP8X4), scales=xs[:, m, :],
                                       in_=xg[m][:].rearrange("p a d t -> p (a d t)"))

@@ -10,29 +10,39 @@ U32 = mybir.dt.uint32
 U8 = mybir.dt.uint8
 ALU = mybir.AluOpType
 ACT = mybir.ActivationFunctionType
-AX = mybir.AxisListType
 
 B, L, D = 16, 512, 128
 P = 128
 NB = L // P
 SCALE = 1.0 / (D ** 0.5)
 FLOPS = 3 * 2 * B * L * L * D
-NMX = 256
+
+XT_AT = -4
+XG_AT = -3
+XQ_AT = 1
+EXP_AT = (1, 6)
+ST_AT = 5
+ET_AT = ((4, 6), (9, 11))
+Q_AT = (8, 13)
+RCP_AT = (8, 13)
+MX_AT = (10, 15)
+LAST = NB * (B - 1) + MX_AT[1]
 
 
 def tile_mutualcrossattention_t_kernel(tc, x1, x2, out):
     nc = tc.nc
     with ExitStack() as ctx:
         keep = ctx.enter_context(tc.tile_pool(name="keep", bufs=1))
+        one = keep
         two = ctx.enter_context(tc.tile_pool(name="two", bufs=2))
         three = ctx.enter_context(tc.tile_pool(name="three", bufs=3))
         psum = ctx.enter_context(tc.psum_pool(name="psum", bufs=2))
 
-        xn = keep.tile([P, 2, B, NB, D], BF16, name="xn")
+        xn = keep.tile([P, B, 2, NB, D], BF16, name="xn")
         cuts = [0, 1, 2, 4, 8, 16]
         for lo, hi in zip(cuts[:-1], cuts[1:]):
-            nc.sync.dma_start(out=xn[:, 0, lo:hi], in_=x1[lo:hi].rearrange("b (p t) d -> p b t d", t=NB))
-            nc.sync.dma_start(out=xn[:, 1, lo:hi], in_=x2[lo:hi].rearrange("b (p t) d -> p b t d", t=NB))
+            nc.sync.dma_start(out=xn[:, lo:hi, 0], in_=x1[lo:hi].rearrange("b (p t) d -> p b t d", t=NB))
+            nc.sync.dma_start(out=xn[:, lo:hi, 1], in_=x2[lo:hi].rearrange("b (p t) d -> p b t d", t=NB))
 
         ident_b = keep.tile([P, P], BF16, name="ident_b")
         make_identity(nc, ident_b[:])
@@ -41,12 +51,11 @@ def tile_mutualcrossattention_t_kernel(tc, x1, x2, out):
 
         xw = keep.tile([P, B, 2 * D], U32, name="xw", align_bytes=64)
         xs = keep.tile([P, B, 2 * D], U8, name="xs", align_bytes=64)
-        nma = keep.tile([P, B, NB], F32, name="nma")
-        nmb = keep.tile([P, B, NB], F32, name="nmb")
-        sums = keep.tile([P, B, 2, NB], F32, name="sums")
-        rcp = keep.tile([P, B, 2, NB], F32, name="rcp")
+        low = keep.tile([P, 2, B, NB], F32, name="low")
+        sums = keep.tile([P, 2, B, NB], F32, name="sums")
+        rcp = keep.tile([P, 2, B, NB], F32, name="rcp")
 
-        xT, xg, sn, stn, ee, grouped, words, planes, tmp, osb = {}, {}, {}, {}, {}, {}, {}, {}, {}, {}
+        xT, xg, neg, ee, grouped, words, planes, scaled, osb = {}, {}, {}, {}, {}, {}, {}, {}, {}
         bank = {}
 
         def at(g, first):
@@ -57,117 +66,62 @@ def tile_mutualcrossattention_t_kernel(tc, x1, x2, out):
             m, q = divmod(g - first, NB)
             return (m, q) if 0 <= m < B else None
 
-        ST_AT = 5
-        MX_AT = 14
-        XQ_AT = 6
-        plan = [(0, 0, 4, 8, "S"), (0, 1, 6, 8, "S"), (1, 0, 9, 13, "S"), (1, 1, 11, 13, "V")]
-
-        def copy_out(engine, dst, src):
-            if engine == "S":
-                nc.scalar.copy(out=dst, in_=src)
-            else:
-                nc.vector.tensor_copy(out=dst, in_=src)
+        def halves(g):
+            return [(side, h, at(g, ET_AT[side][h])) for side in range(2) for h in range(2)
+                    if at(g, ET_AT[side][h]) is not None]
 
         def tensor_engine(g):
-            st, sc, mx = split(g, ST_AT), split(g, 0), split(g, MX_AT)
+            st, sc = split(g, ST_AT), split(g, 0)
             if st is not None:
                 m, u = st
                 bank[("st", g)] = psum.tile([P, L], F32, tag="st", name="st_ps")
                 for t in range(NB):
-                    nc.tensor.transpose(out=bank[("st", g)][:, t * P:(t + 1) * P], in_=sn[m][:, t, u * P:(u + 1) * P],
-                                        identity=ident_f[:])
-            for side, h, et, qz, eng in plan:
-                m = at(g, et)
-                if m is not None:
-                    bank[("et", g)] = psum.tile([P, 2, 2, P], F32, tag="et", name="et_ps")
-                    for r in range(2):
-                        pairs = ee[(side, m)][:, 2 * h + r, :].bitcast(F32)
-                        for u in range(2):
-                            nc.tensor.transpose(out=bank[("et", g)][:, r, u, :], in_=pairs[:, u * P:(u + 1) * P],
-                                                identity=ident_f[:])
+                    nc.tensor.transpose(out=bank[("st", g)][:, t * P:(t + 1) * P],
+                                        in_=neg[(0, m)][:, t, u * P:(u + 1) * P], identity=ident_f[:])
+            for side, h, m in halves(g):
+                bank[("et", g)] = psum.tile([P, 2, 2, P], F32, tag="et", name="et_ps")
+                for r in range(2):
+                    pairs = ee[(side, m)][:, 2 * h + r, :].bitcast(F32)
+                    for u in range(2):
+                        nc.tensor.transpose(out=bank[("et", g)][:, r, u, :], in_=pairs[:, u * P:(u + 1) * P],
+                                            identity=ident_f[:])
+            m = at(g, XT_AT)
+            if m is not None:
+                bank[("x", g)] = psum.tile([P, 2, NB, P], BF16, tag="o", name="xt_ps")
+                for a in range(2):
+                    for t in range(NB):
+                        nc.tensor.transpose(out=bank[("x", g)][:, a, t, :], in_=xn[:, m, a, t, :], identity=ident_b[:])
             hw = L // 2
             if sc is not None:
                 m, t = sc
                 bank[("s", g)] = psum.tile([P, L], F32, tag="s", name="s_ps")
                 nc.tensor.matmul(out=bank[("s", g)][:, 0:hw], lhsT=xT[m][:, 0, t * P:(t + 1) * P],
                                  rhs=xT[m][:, 1, 0:hw], start=True, stop=True)
-            if mx is not None:
-                m, q = mx
-                bank[("o", g)] = psum.tile([P, 2, NMX], F32, tag="o", name="acc")
-                for side in range(2):
-                    lo = 0 if NMX == 2 * D else (1 - side) * D
-                    nc.tensor.matmul_mx(out=bank[("o", g)][:, side, :],
-                                        lhsT=words[(side, m)][:, q * P:(q + 1) * P].bitcast(FP8X4),
-                                        lhsT_scale=planes[(side, m)][:, q * P:(q + 1) * P],
-                                        rhs=xw[:, m, lo:lo + NMX].bitcast(FP8X4),
-                                        rhs_scale=xs[:, m, lo:lo + NMX], start=True, stop=True)
+            for side in range(2):
+                m = at(g, MX_AT[side])
+                if m is not None:
+                    bank[("o", g)] = psum.tile([P, NB, D], F32, tag="o", name="acc")
+                    lo = (1 - side) * D
+                    for q in range(NB):
+                        nc.tensor.matmul_mx(out=bank[("o", g)][:, q, :],
+                                            lhsT=words[(side, m)][:, q * P:(q + 1) * P].bitcast(FP8X4),
+                                            lhsT_scale=planes[(side, m)][:, q * P:(q + 1) * P],
+                                            rhs=xw[:, m, lo:lo + D].bitcast(FP8X4),
+                                            rhs_scale=xs[:, m, lo:lo + D], start=True, stop=True)
             if sc is not None:
                 m, t = sc
                 nc.tensor.matmul(out=bank[("s", g)][:, hw:L], lhsT=xT[m][:, 0, t * P:(t + 1) * P],
                                  rhs=xT[m][:, 1, hw:L], start=True, stop=True)
-            m = at(g, -5)
-            if m is not None:
-                bank[("x", g)] = psum.tile([P, 2, NB, P], BF16, tag="s", name="xt_ps")
-                for a in range(2):
-                    for t in range(NB):
-                        nc.tensor.transpose(out=bank[("x", g)][:, a, t, :], in_=xn[:, a, m, t, :], identity=ident_b[:])
 
-        def copies_out(g):
-            for side, h, et, qz, eng in plan:
-                m = at(g, et)
-                if m is None:
-                    continue
-                if h == 0:
-                    grouped[(side, m)] = two.tile([P, NB, P, NB], BF16, name="grouped%d" % side, align_bytes=64)
-                copy_out(eng, grouped[(side, m)][:, 2 * h:2 * h + 2].bitcast(F32),
-                         bank[("et", g)][:].rearrange("p r u m -> p r m u"))
-
-        def scale_a(g):
-            mx = split(g, MX_AT)
-            if mx is not None:
-                m, q = mx
-                lo = D if NMX == 2 * D else 0
-                tmp[(m, q)] = three.tile([P, D], F32, name="tmp")
-                nc.scalar.activation(out=tmp[(m, q)][:], in_=bank[("o", g)][:, 0, lo:lo + D], func=ACT.Copy,
-                                     scale=rcp[:, m, 0, q:q + 1])
-
-        def minima(g):
-            st, sc = split(g, ST_AT), split(g, 0)
-            if st is not None:
-                m, u = st
-                if u == 0:
-                    stn[m] = three.tile([P, NB, L], F32, name="stn")
-                nc.vector.tensor_scalar(out=stn[m][:, u, :], in0=bank[("st", g)][:], scalar1=1.0, scalar2=None,
-                                        op0=ALU.mult, op1=ALU.min, accum_out=nmb[:, m, u:u + 1])
-            if sc is not None:
-                m, t = sc
-                if t == 0:
-                    sn[m] = three.tile([P, NB, L], F32, name="sn")
-                nc.vector.tensor_scalar(out=sn[m][:, t, :], in0=bank[("s", g)][:], scalar1=-SCALE, scalar2=None,
-                                        op0=ALU.mult, op1=ALU.min, accum_out=nma[:, m, t:t + 1])
-
-        def exps(g):
-            for side, first, src, low in ((0, 1, sn, nma), (1, ST_AT + 1, stn, nmb)):
-                e = split(g, first)
-                if e is not None:
-                    m, t = e
-                    if t == 0:
-                        ee[(side, m)] = three.tile([P, NB, L], BF16, name="ee%d" % side)
-                    nc.scalar.activation(out=ee[(side, m)][:, t, :].rearrange("p (u q e) -> p u q e", u=2, e=2),
-                                         in_=src[m][:, t, :].rearrange("p (u e q) -> p u q e", u=2, e=2), func=ACT.Exp,
-                                         bias=low[:, m, t:t + 1], scale=-1.0, accum_out=sums[:, m, side, t:t + 1])
-
-        def gpsimd(g):
-            m = at(g, 3)
-            if m is not None:
-                xg[m] = two.tile([P, 2, D, NB], BF16, name="xg", align_bytes=64)
-                nc.gpsimd.tensor_scalar(out=xg[m][:], in0=xn[:, :, m].rearrange("p a t d -> p a d t"),
-                                        scalar1=1.0, scalar2=0.0, op0=ALU.mult, op1=ALU.add)
-
-        def quantises(g):
-            for side, h, et, qz, eng in plan:
-                m = at(g, qz)
-                if m is not None and h == 1:
+        def vector_first(g):
+            for side in range(2):
+                m = at(g, MX_AT[side])
+                if m is not None:
+                    scaled[(side, m)] = two.tile([P, NB, D], F32, name="scaled%d" % side)
+                    nc.vector.tensor_tensor(out=scaled[(side, m)][:], in0=bank[("o", g)][:],
+                                            in1=rcp[:, side, m, :].unsqueeze(2).to_broadcast([P, NB, D]), op=ALU.mult)
+                m = at(g, Q_AT[side])
+                if m is not None:
                     words[(side, m)] = three.tile([P, L], U32, name="words%d" % side, align_bytes=64)
                     planes[(side, m)] = three.tile([P, L], U8, name="planes%d" % side, align_bytes=64)
                     nc.vector.quantize_mx(out=words[(side, m)][:].bitcast(FP8X4), scales=planes[(side, m)][:],
@@ -177,35 +131,57 @@ def tile_mutualcrossattention_t_kernel(tc, x1, x2, out):
                 nc.vector.quantize_mx(out=xw[:, m, :].bitcast(FP8X4), scales=xs[:, m, :],
                                       in_=xg[m][:].rearrange("p a d t -> p (a d t)"))
 
-        def scale_b_add(g):
-            mx = split(g, MX_AT)
-            if mx is not None:
-                m, q = mx
-                if q == 0:
-                    osb[m] = three.tile([P, NB, D], F32, name="osb")
-                nc.vector.scalar_tensor_tensor(out=osb[m][:, q, :], in0=bank[("o", g)][:, 1, 0:D],
-                                               scalar=rcp[:, m, 1, q:q + 1], in1=tmp[(m, q)][:],
-                                               op0=ALU.mult, op1=ALU.add)
-                if q == NB - 1:
-                    nc.sync.dma_start(out=out[m].rearrange("(p q) d -> p q d", q=NB), in_=osb[m][:])
+        def minima(g):
+            for side, first, factor, tag in ((1, ST_AT, 1.0, "st"), (0, 0, -SCALE, "s")):
+                e = split(g, first)
+                if e is not None:
+                    m, t = e
+                    if t == 0:
+                        neg[(side, m)] = three.tile([P, NB, L], F32, name="neg%d" % side)
+                    nc.vector.tensor_scalar(out=neg[(side, m)][:, t, :], in0=bank[(tag, g)][:], scalar1=factor,
+                                            scalar2=None, op0=ALU.mult, op1=ALU.min, accum_out=low[:, side, m, t:t + 1])
+            for side in range(2):
+                m = at(g, RCP_AT[side])
+                if m is not None:
+                    nc.vector.reciprocal(out=rcp[:, side, m, :], in_=sums[:, side, m, :])
 
-        def rest(g):
-            m = at(g, -5)
+        def scalar_engine(g):
+            for side, h, m in halves(g):
+                if h == 0:
+                    grouped[(side, m)] = two.tile([P, NB, P, NB], BF16, name="grouped%d" % side, align_bytes=64)
+                nc.scalar.copy(out=grouped[(side, m)][:, 2 * h:2 * h + 2].bitcast(F32),
+                               in_=bank[("et", g)][:].rearrange("p r u m -> p r m u"))
+            for side in (1, 0):
+                e = split(g, EXP_AT[side])
+                if e is not None:
+                    m, t = e
+                    if t == 0:
+                        ee[(side, m)] = three.tile([P, NB, L], BF16, name="ee%d" % side)
+                    nc.scalar.activation(out=ee[(side, m)][:, t, :].rearrange("p (u q e) -> p u q e", u=2, e=2),
+                                         in_=neg[(side, m)][:, t, :].rearrange("p (u e q) -> p u q e", u=2, e=2),
+                                         func=ACT.Exp, bias=low[:, side, m, t:t + 1], scale=-1.0,
+                                         accum_out=sums[:, side, m, t:t + 1])
+            m = at(g, XT_AT)
             if m is not None:
                 xT[m] = three.tile([P, 2, L], BF16, name="xT")
                 nc.scalar.copy(out=xT[m][:], in_=bank[("x", g)][:].rearrange("p a t m -> p a (t m)"))
-            m = at(g, MX_AT - 1)
+
+        def gpsimd(g):
+            m = at(g, XG_AT)
             if m is not None:
-                nc.vector.reciprocal(out=rcp[:, m], in_=sums[:, m])
+                xg[m] = one.tile([P, 2, D, NB], BF16, name="xg", align_bytes=64)
+                nc.gpsimd.tensor_scalar(out=xg[m][:], in0=xn[:, m].rearrange("p a t d -> p a d t"),
+                                        scalar1=1.0, scalar2=0.0, op0=ALU.mult, op1=ALU.add)
+            m = at(g, MX_AT[1])
+            if m is not None:
+                osb[m] = three.tile([P, NB, D], F32, name="osb")
+                nc.gpsimd.tensor_tensor(out=osb[m][:], in0=scaled[(0, m)][:], in1=scaled[(1, m)][:], op=ALU.add)
+                nc.sync.dma_start(out=out[m].rearrange("(p q) d -> p q d", q=NB), in_=osb[m][:])
 
         ctx.enter_context(tc.manual_schedule())
-        for g in range(-5, NB * (B - 1) + MX_AT + NB):
+        for g in range(XT_AT, LAST + 1):
             tensor_engine(g)
-            copies_out(g)
-            scale_a(g)
+            vector_first(g)
             minima(g)
-            exps(g)
+            scalar_engine(g)
             gpsimd(g)
-            quantises(g)
-            scale_b_add(g)
-            rest(g)

@@ -10,6 +10,7 @@ U32 = mybir.dt.uint32
 U8 = mybir.dt.uint8
 ALU = mybir.AluOpType
 ACT = mybir.ActivationFunctionType
+AX = mybir.AxisListType
 
 B, L, D = 16, 512, 128
 P = 128
@@ -20,7 +21,7 @@ FLOPS = 3 * 2 * B * L * L * D
 XT_AT = -4
 XG_AT = -3
 XQ_AT = 1
-EXP_AT = (1, 6)
+EXP_AT = (1, 5)
 ST_AT = 5
 ET_AT = ((4, 6), (9, 11))
 Q_AT = (8, 13)
@@ -131,15 +132,20 @@ def tile_mutualcrossattention_t_kernel(tc, x1, x2, out):
                 nc.vector.quantize_mx(out=xw[:, m, :].bitcast(FP8X4), scales=xs[:, m, :],
                                       in_=xg[m][:].rearrange("p a d t -> p (a d t)"))
 
+        def column_minima(g):
+            e = split(g, ST_AT)
+            if e is not None:
+                m, t = e
+                nc.vector.tensor_reduce(out=low[:, 1, m, t:t + 1], in_=bank[("st", g)][:], axis=AX.X, op=ALU.min)
+
         def minima(g):
-            for side, first, factor, tag in ((1, ST_AT, 1.0, "st"), (0, 0, -SCALE, "s")):
-                e = split(g, first)
-                if e is not None:
-                    m, t = e
-                    if t == 0:
-                        neg[(side, m)] = three.tile([P, NB, L], F32, name="neg%d" % side)
-                    nc.vector.tensor_scalar(out=neg[(side, m)][:, t, :], in0=bank[(tag, g)][:], scalar1=factor,
-                                            scalar2=None, op0=ALU.mult, op1=ALU.min, accum_out=low[:, side, m, t:t + 1])
+            e = split(g, 0)
+            if e is not None:
+                m, t = e
+                if t == 0:
+                    neg[(0, m)] = three.tile([P, NB, L], F32, name="neg0")
+                nc.vector.tensor_scalar(out=neg[(0, m)][:, t, :], in0=bank[("s", g)][:], scalar1=-SCALE,
+                                        scalar2=None, op0=ALU.mult, op1=ALU.min, accum_out=low[:, 0, m, t:t + 1])
             for side in range(2):
                 m = at(g, RCP_AT[side])
                 if m is not None:
@@ -151,14 +157,14 @@ def tile_mutualcrossattention_t_kernel(tc, x1, x2, out):
                     grouped[(side, m)] = two.tile([P, NB, P, NB], BF16, name="grouped%d" % side, align_bytes=64)
                 nc.scalar.copy(out=grouped[(side, m)][:, 2 * h:2 * h + 2].bitcast(F32),
                                in_=bank[("et", g)][:].rearrange("p r u m -> p r m u"))
-            for side in (1, 0):
+            for side in (0, 1):
                 e = split(g, EXP_AT[side])
                 if e is not None:
                     m, t = e
                     if t == 0:
                         ee[(side, m)] = three.tile([P, NB, L], BF16, name="ee%d" % side)
                     nc.scalar.activation(out=ee[(side, m)][:, t, :].rearrange("p (u q e) -> p u q e", u=2, e=2),
-                                         in_=neg[(side, m)][:, t, :].rearrange("p (u e q) -> p u q e", u=2, e=2),
+                                         in_=(neg[(0, m)][:, t, :] if side == 0 else bank[("st", g)][:]).rearrange("p (u e q) -> p u q e", u=2, e=2),
                                          func=ACT.Exp, bias=low[:, side, m, t:t + 1], scale=-1.0,
                                          accum_out=sums[:, side, m, t:t + 1])
             m = at(g, XT_AT)
@@ -181,6 +187,7 @@ def tile_mutualcrossattention_t_kernel(tc, x1, x2, out):
         ctx.enter_context(tc.manual_schedule())
         for g in range(XT_AT, LAST + 1):
             tensor_engine(g)
+            column_minima(g)
             vector_first(g)
             minima(g)
             scalar_engine(g)

@@ -114,13 +114,16 @@ def tile_mutualcrossattention_t_kernel(tc, x1, x2, out):
                 nc.tensor.matmul(out=bank[("s", g)][:, hw:L], lhsT=xT[m][:, 0, t * P:(t + 1) * P],
                                  rhs=xT[m][:, 1, hw:L], start=True, stop=True)
 
-        def vector_first(g):
+        def scalings(g):
             for side in range(2):
                 m = at(g, MX_AT[side])
                 if m is not None:
                     scaled[(side, m)] = two.tile([P, NB, D], F32, name="scaled%d" % side)
                     nc.vector.tensor_tensor(out=scaled[(side, m)][:], in0=bank[("o", g)][:],
                                             in1=rcp[:, side, m, :].unsqueeze(2).to_broadcast([P, NB, D]), op=ALU.mult)
+
+        def quantises(g):
+            for side in range(2):
                 m = at(g, Q_AT[side])
                 if m is not None:
                     words[(side, m)] = three.tile([P, L], U32, name="words%d" % side, align_bytes=64)
@@ -188,7 +191,8 @@ def tile_mutualcrossattention_t_kernel(tc, x1, x2, out):
         for g in range(XT_AT, LAST + 1):
             tensor_engine(g)
             column_minima(g)
-            vector_first(g)
+            scalings(g)
             minima(g)
+            quantises(g)
             scalar_engine(g)
             gpsimd(g)

@@ -117,7 +117,14 @@ def tile_mutualcrossattention_t_kernel(tc, x1, x2, out):
         def scalings(g):
             for side in range(2):
                 m = at(g, MX_AT[side])
-                if m is not None:
+                if m is not None and side == 1:
+                    osb[m] = three.tile([P, NB, D], F32, name="osb")
+                    for q in range(NB):
+                        nc.vector.scalar_tensor_tensor(out=osb[m][:, q, :], in0=bank[("o", g)][:, q, :],
+                                                       scalar=rcp[:, 1, m, q:q + 1], in1=scaled[(0, m)][:, q, :],
+                                                       op0=ALU.mult, op1=ALU.add)
+                    nc.sync.dma_start(out=out[m].rearrange("(p q) d -> p q d", q=NB), in_=osb[m][:])
+                elif m is not None:
                     scaled[(side, m)] = two.tile([P, NB, D], F32, name="scaled%d" % side)
                     nc.vector.tensor_tensor(out=scaled[(side, m)][:], in0=bank[("o", g)][:],
                                             in1=rcp[:, side, m, :].unsqueeze(2).to_broadcast([P, NB, D]), op=ALU.mult)
@@ -181,11 +188,6 @@ def tile_mutualcrossattention_t_kernel(tc, x1, x2, out):
                 xg[m] = one.tile([P, 2, D, NB], BF16, name="xg", align_bytes=64)
                 nc.gpsimd.tensor_scalar(out=xg[m][:], in0=xn[:, m].rearrange("p a t d -> p a d t"),
                                         scalar1=1.0, scalar2=0.0, op0=ALU.mult, op1=ALU.add)
-            m = at(g, MX_AT[1])
-            if m is not None:
-                osb[m] = three.tile([P, NB, D], F32, name="osb")
-                nc.gpsimd.tensor_tensor(out=osb[m][:], in0=scaled[(0, m)][:], in1=scaled[(1, m)][:], op=ALU.add)
-                nc.sync.dma_start(out=out[m].rearrange("(p q) d -> p q d", q=NB), in_=osb[m][:])
 
         ctx.enter_context(tc.manual_schedule())
         for g in range(XT_AT, LAST + 1):

@@ -25,8 +25,10 @@ EXP_AT = (1, 5)
 ST_AT = 5
 ET_AT = ((4, 6), (9, 11))
 Q_AT = (8, 13)
-RCP_AT = (8, 13)
+RCP_AT = 8
 MX_AT = (10, 15)
+END_Q_AT = (10, 12)
+END_MX_AT = (13, 14)
 LAST = NB * (B - 1) + MX_AT[1]
 
 
@@ -53,8 +55,8 @@ def tile_mutualcrossattention_t_kernel(tc, x1, x2, out):
         xw = keep.tile([P, B, 2 * D], U32, name="xw", align_bytes=64)
         xs = keep.tile([P, B, 2 * D], U8, name="xs", align_bytes=64)
         low = keep.tile([P, 2, B, NB], F32, name="low")
-        sums = keep.tile([P, 2, B, NB], F32, name="sums")
-        rcp = keep.tile([P, 2, B, NB], F32, name="rcp")
+        sums = keep.tile([P, B, 2, NB], F32, name="sums")
+        rcp = keep.tile([P, B, 2, NB], F32, name="rcp")
 
         xT, xg, neg, ee, grouped, words, planes, scaled, osb = {}, {}, {}, {}, {}, {}, {}, {}, {}
         bank = {}
@@ -70,6 +72,20 @@ def tile_mutualcrossattention_t_kernel(tc, x1, x2, out):
         def halves(g):
             return [(side, h, at(g, ET_AT[side][h])) for side in range(2) for h in range(2)
                     if at(g, ET_AT[side][h]) is not None]
+
+        def by_halves(g, whole, halved):
+            found = []
+            for side in range(2):
+                m = at(g, whole[side])
+                if m is not None and (side, m) != (1, B - 1):
+                    found.append((side, m, (0, 1, 2, 3)))
+            for h in range(2):
+                if g == NB * (B - 1) + halved[h]:
+                    found.append((1, B - 1, (2 * h, 2 * h + 1)))
+            return found
+
+        def products(g):
+            return by_halves(g, MX_AT, END_MX_AT)
 
         def tensor_engine(g):
             st, sc = split(g, ST_AT), split(g, 0)
@@ -98,45 +114,46 @@ def tile_mutualcrossattention_t_kernel(tc, x1, x2, out):
                 bank[("s", g)] = psum.tile([P, L], F32, tag="s", name="s_ps")
                 nc.tensor.matmul(out=bank[("s", g)][:, 0:hw], lhsT=xT[m][:, 0, t * P:(t + 1) * P],
                                  rhs=xT[m][:, 1, 0:hw], start=True, stop=True)
-            for side in range(2):
-                m = at(g, MX_AT[side])
-                if m is not None:
-                    bank[("o", g)] = psum.tile([P, NB, D], F32, tag="o", name="acc")
-                    lo = (1 - side) * D
-                    for q in range(NB):
-                        nc.tensor.matmul_mx(out=bank[("o", g)][:, q, :],
-                                            lhsT=words[(side, m)][:, q * P:(q + 1) * P].bitcast(FP8X4),
-                                            lhsT_scale=planes[(side, m)][:, q * P:(q + 1) * P],
-                                            rhs=xw[:, m, lo:lo + D].bitcast(FP8X4),
-                                            rhs_scale=xs[:, m, lo:lo + D], start=True, stop=True)
+            for side, m, tiles in products(g):
+                if tiles[0] == 0:
+                    bank[("o", side, m)] = psum.tile([P, NB, D], F32, tag="o", name="acc")
+                lo = (1 - side) * D
+                for q in tiles:
+                    nc.tensor.matmul_mx(out=bank[("o", side, m)][:, q, :],
+                                        lhsT=words[(side, m)][:, q * P:(q + 1) * P].bitcast(FP8X4),
+                                        lhsT_scale=planes[(side, m)][:, q * P:(q + 1) * P],
+                                        rhs=xw[:, m, lo:lo + D].bitcast(FP8X4),
+                                        rhs_scale=xs[:, m, lo:lo + D], start=True, stop=True)
             if sc is not None:
                 m, t = sc
                 nc.tensor.matmul(out=bank[("s", g)][:, hw:L], lhsT=xT[m][:, 0, t * P:(t + 1) * P],
                                  rhs=xT[m][:, 1, hw:L], start=True, stop=True)
 
         def scalings(g):
-            for side in range(2):
-                m = at(g, MX_AT[side])
-                if m is not None and side == 1:
-                    osb[m] = three.tile([P, NB, D], F32, name="osb")
-                    for q in range(NB):
-                        nc.vector.scalar_tensor_tensor(out=osb[m][:, q, :], in0=bank[("o", g)][:, q, :],
-                                                       scalar=rcp[:, 1, m, q:q + 1], in1=scaled[(0, m)][:, q, :],
+            for side, m, tiles in products(g):
+                if side == 0:
+                    scaled[m] = two.tile([P, NB, D], F32, name="scaled")
+                    nc.vector.tensor_tensor(out=scaled[m][:], in0=bank[("o", 0, m)][:],
+                                            in1=rcp[:, m, 0, :].unsqueeze(2).to_broadcast([P, NB, D]), op=ALU.mult)
+                else:
+                    if tiles[0] == 0:
+                        osb[m] = three.tile([P, NB, D], F32, name="osb")
+                    for q in tiles:
+                        nc.vector.scalar_tensor_tensor(out=osb[m][:, q, :], in0=bank[("o", 1, m)][:, q, :],
+                                                       scalar=rcp[:, m, 1, q:q + 1], in1=scaled[m][:, q, :],
                                                        op0=ALU.mult, op1=ALU.add)
-                    nc.sync.dma_start(out=out[m].rearrange("(p q) d -> p q d", q=NB), in_=osb[m][:])
-                elif m is not None:
-                    scaled[(side, m)] = two.tile([P, NB, D], F32, name="scaled%d" % side)
-                    nc.vector.tensor_tensor(out=scaled[(side, m)][:], in0=bank[("o", g)][:],
-                                            in1=rcp[:, side, m, :].unsqueeze(2).to_broadcast([P, NB, D]), op=ALU.mult)
+                    lo, hi = tiles[0], tiles[-1] + 1
+                    nc.sync.dma_start(out=out[m].rearrange("(p q) d -> p q d", q=NB)[:, lo:hi, :], in_=osb[m][:, lo:hi, :])
 
         def quantises(g):
-            for side in range(2):
-                m = at(g, Q_AT[side])
-                if m is not None:
+            for side, m, tiles in by_halves(g, Q_AT, END_Q_AT):
+                if tiles[0] == 0:
                     words[(side, m)] = three.tile([P, L], U32, name="words%d" % side, align_bytes=64)
                     planes[(side, m)] = three.tile([P, L], U8, name="planes%d" % side, align_bytes=64)
-                    nc.vector.quantize_mx(out=words[(side, m)][:].bitcast(FP8X4), scales=planes[(side, m)][:],
-                                          in_=grouped[(side, m)][:].rearrange("p r m c -> p (r m c)"))
+                lo, hi = tiles[0], tiles[-1] + 1
+                nc.vector.quantize_mx(out=words[(side, m)][:, lo * P:hi * P].bitcast(FP8X4),
+                                      scales=planes[(side, m)][:, lo * P:hi * P],
+                                      in_=grouped[(side, m)][:, lo:hi].rearrange("p r m c -> p (r m c)"))
             m = at(g, XQ_AT)
             if m is not None:
                 nc.vector.quantize_mx(out=xw[:, m, :].bitcast(FP8X4), scales=xs[:, m, :],
@@ -156,10 +173,11 @@ def tile_mutualcrossattention_t_kernel(tc, x1, x2, out):
                     neg[(0, m)] = three.tile([P, NB, L], F32, name="neg0")
                 nc.vector.tensor_scalar(out=neg[(0, m)][:, t, :], in0=bank[("s", g)][:], scalar1=-SCALE,
                                         scalar2=None, op0=ALU.mult, op1=ALU.min, accum_out=low[:, 0, m, t:t + 1])
-            for side in range(2):
-                m = at(g, RCP_AT[side])
-                if m is not None:
-                    nc.vector.reciprocal(out=rcp[:, side, m, :], in_=sums[:, side, m, :])
+            m, r = divmod(g - RCP_AT, NB)
+            if r == 0 and 0 <= m <= B:
+                lo, hi = max(0, 2 * NB * m - NB), min(2 * NB * B, 2 * NB * m + NB)
+                nc.vector.reciprocal(out=rcp[:].rearrange("p b s t -> p (b s t)")[:, lo:hi],
+                                     in_=sums[:].rearrange("p b s t -> p (b s t)")[:, lo:hi])
 
         def scalar_engine(g):
             for side, h, m in halves(g):
@@ -176,7 +194,7 @@ def tile_mutualcrossattention_t_kernel(tc, x1, x2, out):
                     nc.scalar.activation(out=ee[(side, m)][:, t, :].rearrange("p (u q e) -> p u q e", u=2, e=2),
                                          in_=(neg[(0, m)][:, t, :] if side == 0 else bank[("st", g)][:]).rearrange("p (u e q) -> p u q e", u=2, e=2),
                                          func=ACT.Exp, bias=low[:, side, m, t:t + 1], scale=-1.0,
-                                         accum_out=sums[:, side, m, t:t + 1])
+                                         accum_out=sums[:, m, side, t:t + 1])
             m = at(g, XT_AT)
             if m is not None:
                 xT[m] = three.tile([P, 2, L], BF16, name="xT")

@@ -30,6 +30,7 @@ MX_AT = (10, 15)
 END_Q_AT = (10, 12)
 END_MX_AT = (13, 14)
 LAST = NB * (B - 1) + MX_AT[1]
+N_WARM = 3
 
 
 def tile_mutualcrossattention_t_kernel(tc, x1, x2, out):
@@ -40,6 +41,12 @@ def tile_mutualcrossattention_t_kernel(tc, x1, x2, out):
         two = ctx.enter_context(tc.tile_pool(name="two", bufs=2))
         three = ctx.enter_context(tc.tile_pool(name="three", bufs=3))
         psum = ctx.enter_context(tc.psum_pool(name="psum", bufs=2))
+
+        idle = keep.tile([P, L], BF16, name="idle")
+        nc.vector.memset(idle[:], 0.0)
+        idle_ps = psum.tile([P, L], F32, tag="s", name="idle_ps")
+        for i in range(N_WARM):
+            nc.tensor.matmul(out=idle_ps[:], lhsT=idle[:, 0:P], rhs=idle[:], start=True, stop=True)
 
         xn = keep.tile([P, B, 2, NB, D], BF16, name="xn")
         cuts = [0, 1, 2, 4, 8, 16]

@@ -44,7 +44,7 @@ def tile_mutualcrossattention_t_kernel(tc, x1, x2, out):
 
         idle = keep.tile([P, L], BF16, name="idle")
         nc.vector.memset(idle[:], 0.0)
-        idle_ps = psum.tile([P, L], F32, tag="s", name="idle_ps")
+        idle_ps = psum.tile([P, L], F32, tag="p", name="idle_ps", bufs=8)
         for i in range(N_WARM):
             nc.tensor.matmul(out=idle_ps[:], lhsT=idle[:, 0:P], rhs=idle[:], start=True, stop=True)
 
@@ -98,12 +98,12 @@ def tile_mutualcrossattention_t_kernel(tc, x1, x2, out):
             st, sc = split(g, ST_AT), split(g, 0)
             if st is not None:
                 m, u = st
-                bank[("st", g)] = psum.tile([P, L], F32, tag="st", name="st_ps")
+                bank[("st", g)] = psum.tile([P, L], F32, tag="p", name="st_ps", bufs=8)
                 for t in range(NB):
                     nc.tensor.transpose(out=bank[("st", g)][:, t * P:(t + 1) * P],
                                         in_=neg[(0, m)][:, t, u * P:(u + 1) * P], identity=ident_f[:])
             for side, h, m in halves(g):
-                bank[("et", g)] = psum.tile([P, 2, 2, P], F32, tag="et", name="et_ps")
+                bank[("et", g)] = psum.tile([P, 2, 2, P], F32, tag="p", name="et_ps", bufs=8)
                 for r in range(2):
                     pairs = ee[(side, m)][:, 2 * h + r, :].bitcast(F32)
                     for u in range(2):
@@ -111,19 +111,19 @@ def tile_mutualcrossattention_t_kernel(tc, x1, x2, out):
                                             identity=ident_f[:])
             m = at(g, XT_AT)
             if m is not None:
-                bank[("x", g)] = psum.tile([P, 2, NB, P], BF16, tag="o", name="xt_ps")
+                bank[("x", g)] = psum.tile([P, 2, NB, P], BF16, tag="p", name="xt_ps", bufs=8)
                 for a in range(2):
                     for t in range(NB):
                         nc.tensor.transpose(out=bank[("x", g)][:, a, t, :], in_=xn[:, m, a, t, :], identity=ident_b[:])
             hw = L // 2
             if sc is not None:
                 m, t = sc
-                bank[("s", g)] = psum.tile([P, L], F32, tag="s", name="s_ps")
+                bank[("s", g)] = psum.tile([P, L], F32, tag="p", name="s_ps", bufs=8)
                 nc.tensor.matmul(out=bank[("s", g)][:, 0:hw], lhsT=xT[m][:, 0, t * P:(t + 1) * P],
                                  rhs=xT[m][:, 1, 0:hw], start=True, stop=True)
             for side, m, tiles in products(g):
                 if tiles[0] == 0:
-                    bank[("o", side, m)] = psum.tile([P, NB, D], F32, tag="o", name="acc")
+                    bank[("o", side, m)] = psum.tile([P, NB, D], F32, tag="p", name="acc", bufs=8)
                 lo = (1 - side) * D
                 for q in tiles:
                     nc.tensor.matmul_mx(out=bank[("o", side, m)][:, q, :],

@@ -18,19 +18,33 @@ NB = L // P
 SCALE = 1.0 / (D ** 0.5)
 FLOPS = 3 * 2 * B * L * L * D
 
-XT_AT = -4
-XG_AT = -3
-XQ_AT = 1
-EXP_AT = (1, 5)
-ST_AT = 5
-ET_AT = ((4, 6), (9, 11))
-Q_AT = (8, 13)
-RCP_AT = 8
-MX_AT = (10, 15)
-END_Q_AT = (10, 12)
-END_MX_AT = (13, 14)
-LAST = NB * (B - 1) + MX_AT[1]
+XT_AT = -5
+XG_AT = 4
+XQ_AT = 8
+GAP_AT = 2
+G_LO = 1
+G_HI = 16
+G_EVERY = 101
+LOW_AT = (5,7,)
+EXP_AT = (1,6,)
+ET_AT = ((4,6,),(9,11,),)
+Q_AT = (8,12,)
+RCP_AT = 7
+MX_AT = (11,17,)
+END_Q_AT = (10,15,)
+END_MX_AT = (12,18,)
+LAST = NB * (B - 1) + max(MX_AT[1] + 1, END_MX_AT[1])
 N_WARM = 3
+S_BUFS = 3
+BIG = 3.0e38
+ORDER = "cmCxXOeQVylRGtAELB"
+E_ON_V = 100
+X_ON_S = 3
+X_EVERY = 6
+MX_INSIDE = False
+ST_BUFS = 2
+ET_BUFS = 1
+O_BUFS = 2
 
 
 def tile_mutualcrossattention_t_kernel(tc, x1, x2, out):
@@ -40,6 +54,7 @@ def tile_mutualcrossattention_t_kernel(tc, x1, x2, out):
         one = keep
         two = ctx.enter_context(tc.tile_pool(name="two", bufs=2))
         three = ctx.enter_context(tc.tile_pool(name="three", bufs=3))
+        four = ctx.enter_context(tc.tile_pool(name="four", bufs=4))
         psum = ctx.enter_context(tc.psum_pool(name="psum", bufs=2))
 
         idle = keep.tile([P, L], BF16, name="idle")
@@ -65,7 +80,7 @@ def tile_mutualcrossattention_t_kernel(tc, x1, x2, out):
         sums = keep.tile([P, B, 2, NB], F32, name="sums")
         rcp = keep.tile([P, B, 2, NB], F32, name="rcp")
 
-        xT, xg, neg, ee, grouped, words, planes, scaled, osb = {}, {}, {}, {}, {}, {}, {}, {}, {}
+        xT, xg, neg, least, ee, grouped, words, planes, scaled, osb = {}, {}, {}, {}, {}, {}, {}, {}, {}, {}
         bank = {}
 
         def at(g, first):
@@ -94,14 +109,31 @@ def tile_mutualcrossattention_t_kernel(tc, x1, x2, out):
         def products(g):
             return by_halves(g, MX_AT, END_MX_AT)
 
-        def tensor_engine(g):
-            st, sc = split(g, ST_AT), split(g, 0)
+        def pe_low(g):
+            for h in range(2):
+                m = at(g, LOW_AT[h])
+                if m is not None and mode(m) == 1:
+                    bank[("low", m, h)] = psum.tile([P, 2, 2, P], F32, tag="p", name="low_ps", bufs=8)
+                    for u in range(2):
+                        cols = slice((2 * h + u) * P, (2 * h + u + 1) * P)
+                        for k in range(2):
+                            nc.tensor.transpose(out=bank[("low", m, h)][:, u, k, :], in_=least[m][:, k, cols], identity=ident_f[:])
+            m = at(g, LOW_AT[0])
+            if m is not None and mode(m) == 0:
+                bank[("low", m, 0)] = psum.tile([P, NB, P], F32, tag="p", name="low_ps", bufs=8)
+                for u in range(NB):
+                    nc.tensor.transpose(out=bank[("low", m, 0)][:, u, :], in_=least[m][:, 0, u * P:(u + 1) * P], identity=ident_f[:])
+
+        def pe_st(g):
+            st = split(g, EXP_AT[1])
             if st is not None:
                 m, u = st
                 bank[("st", g)] = psum.tile([P, L], F32, tag="p", name="st_ps", bufs=8)
                 for t in range(NB):
                     nc.tensor.transpose(out=bank[("st", g)][:, t * P:(t + 1) * P],
-                                        in_=neg[(0, m)][:, t, u * P:(u + 1) * P], identity=ident_f[:])
+                                        in_=neg[m][:, t, u * P:(u + 1) * P], identity=ident_f[:])
+
+        def pe_et(g):
             for side, h, m in halves(g):
                 bank[("et", g)] = psum.tile([P, 2, 2, P], F32, tag="p", name="et_ps", bufs=8)
                 for r in range(2):
@@ -109,18 +141,35 @@ def tile_mutualcrossattention_t_kernel(tc, x1, x2, out):
                     for u in range(2):
                         nc.tensor.transpose(out=bank[("et", g)][:, r, u, :], in_=pairs[:, u * P:(u + 1) * P],
                                             identity=ident_f[:])
+
+        def pe_xt(g):
             m = at(g, XT_AT)
             if m is not None:
                 bank[("x", g)] = psum.tile([P, 2, NB, P], BF16, tag="p", name="xt_ps", bufs=8)
                 for a in range(2):
                     for t in range(NB):
                         nc.tensor.transpose(out=bank[("x", g)][:, a, t, :], in_=xn[:, m, a, t, :], identity=ident_b[:])
+
+        def pe_scores(g):
             hw = L // 2
+            sc = split(g, 0)
             if sc is not None:
                 m, t = sc
                 bank[("s", g)] = psum.tile([P, L], F32, tag="p", name="s_ps", bufs=8)
                 nc.tensor.matmul(out=bank[("s", g)][:, 0:hw], lhsT=xT[m][:, 0, t * P:(t + 1) * P],
                                  rhs=xT[m][:, 1, 0:hw], start=True, stop=True)
+            if MX_INSIDE:
+                pe_mx(g)
+            if sc is not None:
+                m, t = sc
+                nc.tensor.matmul(out=bank[("s", g)][:, hw:L], lhsT=xT[m][:, 0, t * P:(t + 1) * P],
+                                 rhs=xT[m][:, 1, hw:L], start=True, stop=True)
+
+        def pe_m(g):
+            if not MX_INSIDE:
+                pe_mx(g)
+
+        def pe_mx(g):
             for side, m, tiles in products(g):
                 if tiles[0] == 0:
                     bank[("o", side, m)] = psum.tile([P, NB, D], F32, tag="p", name="acc", bufs=8)
@@ -131,15 +180,11 @@ def tile_mutualcrossattention_t_kernel(tc, x1, x2, out):
                                         lhsT_scale=planes[(side, m)][:, q * P:(q + 1) * P],
                                         rhs=xw[:, m, lo:lo + D].bitcast(FP8X4),
                                         rhs_scale=xs[:, m, lo:lo + D], start=True, stop=True)
-            if sc is not None:
-                m, t = sc
-                nc.tensor.matmul(out=bank[("s", g)][:, hw:L], lhsT=xT[m][:, 0, t * P:(t + 1) * P],
-                                 rhs=xT[m][:, 1, hw:L], start=True, stop=True)
 
         def scalings(g):
             for side, m, tiles in products(g):
                 if side == 0:
-                    scaled[m] = two.tile([P, NB, D], F32, name="scaled")
+                    scaled[m] = three.tile([P, NB, D], F32, name="scaled")
                     nc.vector.tensor_tensor(out=scaled[m][:], in0=bank[("o", 0, m)][:],
                                             in1=rcp[:, m, 0, :].unsqueeze(2).to_broadcast([P, NB, D]), op=ALU.mult)
                 else:
@@ -167,45 +212,89 @@ def tile_mutualcrossattention_t_kernel(tc, x1, x2, out):
                                       in_=xg[m][:].rearrange("p a d t -> p (a d t)"))
 
         def column_minima(g):
-            e = split(g, ST_AT)
-            if e is not None:
-                m, t = e
-                nc.vector.tensor_reduce(out=low[:, 1, m, t:t + 1], in_=bank[("st", g)][:], axis=AX.X, op=ALU.min)
+            for h in range(2):
+                m = at(g, LOW_AT[h])
+                if m is not None and mode(m) == 1:
+                    nc.vector.tensor_reduce(out=low[:, 1, m, 2 * h:2 * h + 2], in_=bank[("low", m, h)][:].rearrange("p u k c -> p u (k c)"),
+                                            axis=AX.X, op=ALU.min)
+            m = at(g, LOW_AT[0])
+            if m is not None and mode(m) == 0:
+                nc.vector.tensor_reduce(out=low[:, 1, m, :], in_=bank[("low", m, 0)][:], axis=AX.X, op=ALU.min)
 
-        def minima(g):
+        def mode(m):
+            return 1 if G_LO <= m < G_HI and m % G_EVERY != G_EVERY - 1 else 0
+
+        def x_copy(g):
+            m = at(g, XT_AT)
+            if m is not None and m >= X_ON_S and m % X_EVERY != 1:
+                do_x_copy(g, m, nc.vector.tensor_copy)
+
+        def x_copy_s(g):
+            m = at(g, XT_AT)
+            if m is not None and not (m >= X_ON_S and m % X_EVERY != 1):
+                do_x_copy(g, m, nc.scalar.copy)
+
+        def do_x_copy(g, m, copy):
+            if True:
+                xT[m] = three.tile([P, 2, L], BF16, name="xT")
+                copy(out=xT[m][:], in_=bank[("x", g)][:].rearrange("p a t m -> p a (t m)"))
+
+        def copies(g):
             e = split(g, 0)
             if e is not None:
                 m, t = e
                 if t == 0:
-                    neg[(0, m)] = three.tile([P, NB, L], F32, name="neg0")
-                nc.vector.tensor_scalar(out=neg[(0, m)][:, t, :], in0=bank[("s", g)][:], scalar1=-SCALE,
+                    neg[m] = four.tile([P, NB, L], F32, name="neg0")
+                nc.vector.tensor_scalar(out=neg[m][:, t, :], in0=bank[("s", g)][:], scalar1=-SCALE,
                                         scalar2=None, op0=ALU.mult, op1=ALU.min, accum_out=low[:, 0, m, t:t + 1])
+                if t == 0:
+                    least[m] = two.tile([P, 2, L], F32, name="least")
+                if mode(m) == 0 and t > 0:
+                    nc.vector.scalar_tensor_tensor(out=least[m][:, 0, :], in0=bank[("s", g)][:], scalar=-SCALE,
+                                                   in1=neg[m][:, 0, :] if t == 1 else least[m][:, 0, :], op0=ALU.mult, op1=ALU.min)
+                if mode(m) == 1 and t == 3:
+                    nc.vector.scalar_tensor_tensor(out=least[m][:, 1, :], in0=bank[("s", g)][:], scalar=-SCALE,
+                                                   in1=neg[m][:, 2, :], op0=ALU.mult, op1=ALU.min)
+
+        def reciprocals(g):
             m, r = divmod(g - RCP_AT, NB)
             if r == 0 and 0 <= m <= B:
                 lo, hi = max(0, 2 * NB * m - NB), min(2 * NB * B, 2 * NB * m + NB)
                 nc.vector.reciprocal(out=rcp[:].rearrange("p b s t -> p (b s t)")[:, lo:hi],
                                      in_=sums[:].rearrange("p b s t -> p (b s t)")[:, lo:hi])
 
-        def scalar_engine(g):
+        def s_copy(g):
+            if g < E_ON_V:
+                e_copy(g, nc.scalar.copy)
+
+        def v_copy(g):
+            if g >= E_ON_V:
+                e_copy(g, nc.vector.tensor_copy)
+
+        def e_copy(g, copy):
             for side, h, m in halves(g):
                 if h == 0:
                     grouped[(side, m)] = two.tile([P, NB, P, NB], BF16, name="grouped%d" % side, align_bytes=64)
-                nc.scalar.copy(out=grouped[(side, m)][:, 2 * h:2 * h + 2].bitcast(F32),
-                               in_=bank[("et", g)][:].rearrange("p r u m -> p r m u"))
-            for side in (0, 1):
+                copy(out=grouped[(side, m)][:, 2 * h:2 * h + 2].bitcast(F32),
+                     in_=bank[("et", g)][:].rearrange("p r u m -> p r m u"))
+
+        def s_a(g):
+            exps(g, 0)
+
+        def s_b(g):
+            exps(g, 1)
+
+        def exps(g, side):
+            if True:
                 e = split(g, EXP_AT[side])
                 if e is not None:
                     m, t = e
                     if t == 0:
                         ee[(side, m)] = three.tile([P, NB, L], BF16, name="ee%d" % side)
                     nc.scalar.activation(out=ee[(side, m)][:, t, :].rearrange("p (u q e) -> p u q e", u=2, e=2),
-                                         in_=(neg[(0, m)][:, t, :] if side == 0 else bank[("st", g)][:]).rearrange("p (u e q) -> p u q e", u=2, e=2),
+                                         in_=(neg[m][:, t, :] if side == 0 else bank[("st", g)][:]).rearrange("p (u e q) -> p u q e", u=2, e=2),
                                          func=ACT.Exp, bias=low[:, side, m, t:t + 1], scale=-1.0,
                                          accum_out=sums[:, m, side, t:t + 1])
-            m = at(g, XT_AT)
-            if m is not None:
-                xT[m] = three.tile([P, 2, L], BF16, name="xT")
-                nc.scalar.copy(out=xT[m][:], in_=bank[("x", g)][:].rearrange("p a t m -> p a (t m)"))
 
         def gpsimd(g):
             m = at(g, XG_AT)
@@ -213,13 +302,17 @@ def tile_mutualcrossattention_t_kernel(tc, x1, x2, out):
                 xg[m] = one.tile([P, 2, D, NB], BF16, name="xg", align_bytes=64)
                 nc.gpsimd.tensor_scalar(out=xg[m][:], in0=xn[:, m].rearrange("p a t d -> p a d t"),
                                         scalar1=1.0, scalar2=0.0, op0=ALU.mult, op1=ALU.add)
+            m = at(g, GAP_AT)
+            if m is not None and mode(m) == 1:
+                nc.gpsimd.tensor_tensor(out=least[m][:, 0, :], in0=neg[m][:, 0, :], in1=neg[m][:, 1, :], op=ALU.subtract)
+                nc.gpsimd.tensor_scalar(out=least[m][:, 0, :], in0=least[m][:, 0, :], scalar1=0.0, scalar2=-BIG,
+                                        op0=ALU.min, op1=ALU.max)
+                nc.gpsimd.tensor_tensor(out=least[m][:, 0, :], in0=least[m][:, 0, :], in1=neg[m][:, 1, :], op=ALU.add)
 
         ctx.enter_context(tc.manual_schedule())
         for g in range(XT_AT, LAST + 1):
-            tensor_engine(g)
-            column_minima(g)
-            scalings(g)
-            minima(g)
-            quantises(g)
-            scalar_engine(g)
-            gpsimd(g)
+            tasks = {"e": pe_et, "x": pe_xt, "c": pe_scores, "l": pe_low, "t": pe_st, "m": pe_m,
+                     "C": copies, "L": column_minima, "X": x_copy, "O": scalings, "R": reciprocals, "Q": quantises,
+                     "E": s_copy, "A": s_a, "B": s_b, "G": gpsimd, "y": x_copy_s, "V": v_copy}
+            for k in ORDER:
+                tasks[k](g)

@@ -19,12 +19,13 @@ SCALE = 1.0 / (D ** 0.5)
 FLOPS = 3 * 2 * B * L * L * D
 
 XT_AT = -5
+XT_LAG = -100
 XG_AT = 4
 XQ_AT = 8
-GAP_AT = 2
+GAP_AT = (2,4,)
 G_LO = 1
 G_HI = 16
-G_EVERY = 101
+G_EVERY = 1
 LOW_AT = (5,7,)
 EXP_AT = (1,6,)
 ET_AT = ((4,6,),(9,11,),)
@@ -34,6 +35,7 @@ MX_AT = (11,17,)
 END_Q_AT = (10,15,)
 END_MX_AT = (12,18,)
 LAST = NB * (B - 1) + max(MX_AT[1] + 1, END_MX_AT[1])
+PIECES = ((0, 1), (2, 3))
 N_WARM = 3
 S_BUFS = 3
 BIG = 3.0e38
@@ -54,6 +56,7 @@ def tile_mutualcrossattention_t_kernel(tc, x1, x2, out):
         one = keep
         two = ctx.enter_context(tc.tile_pool(name="two", bufs=2))
         three = ctx.enter_context(tc.tile_pool(name="three", bufs=3))
+        six = ctx.enter_context(tc.tile_pool(name="six", bufs=6))
         four = ctx.enter_context(tc.tile_pool(name="four", bufs=4))
         psum = ctx.enter_context(tc.psum_pool(name="psum", bufs=2))
 
@@ -87,6 +90,10 @@ def tile_mutualcrossattention_t_kernel(tc, x1, x2, out):
             m, r = divmod(g - first, NB)
             return m if (r == 0 and 0 <= m < B) else None
 
+        def x_at(g):
+            found = [m for m in range(B) if (XT_AT if m == 0 else max(m - 1 + XT_LAG, XT_AT + 4 * m)) == g]
+            return found[0] if found else None
+
         def split(g, first):
             m, q = divmod(g - first, NB)
             return (m, q) if 0 <= m < B else None
@@ -101,9 +108,9 @@ def tile_mutualcrossattention_t_kernel(tc, x1, x2, out):
                 m = at(g, whole[side])
                 if m is not None and (side, m) != (1, B - 1):
                     found.append((side, m, (0, 1, 2, 3)))
-            for h in range(2):
+            for h in range(len(PIECES)):
                 if g == NB * (B - 1) + halved[h]:
-                    found.append((1, B - 1, (2 * h, 2 * h + 1)))
+                    found.append((1, B - 1, PIECES[h]))
             return found
 
         def products(g):
@@ -112,12 +119,16 @@ def tile_mutualcrossattention_t_kernel(tc, x1, x2, out):
         def pe_low(g):
             for h in range(2):
                 m = at(g, LOW_AT[h])
-                if m is not None and mode(m) == 1:
+                if m is not None and mode(m) > 0:
                     bank[("low", m, h)] = psum.tile([P, 2, 2, P], F32, tag="p", name="low_ps", bufs=8)
                     for u in range(2):
                         cols = slice((2 * h + u) * P, (2 * h + u + 1) * P)
                         for k in range(2):
-                            nc.tensor.transpose(out=bank[("low", m, h)][:, u, k, :], in_=least[m][:, k, cols], identity=ident_f[:])
+                            if mode(m) == 2 or k == 0:
+                                nc.tensor.matmul(out=bank[("low", m, h)][:, u, k, :], lhsT=neg[m][:, 2 * k + 1, cols], rhs=ident_f[:], start=True, stop=False, is_transpose=True)
+                                nc.tensor.matmul(out=bank[("low", m, h)][:, u, k, :], lhsT=least[m][:, k, cols], rhs=ident_f[:], start=False, stop=True, is_transpose=True)
+                            else:
+                                nc.tensor.transpose(out=bank[("low", m, h)][:, u, k, :], in_=least[m][:, k, cols], identity=ident_f[:])
             m = at(g, LOW_AT[0])
             if m is not None and mode(m) == 0:
                 bank[("low", m, 0)] = psum.tile([P, NB, P], F32, tag="p", name="low_ps", bufs=8)
@@ -143,7 +154,7 @@ def tile_mutualcrossattention_t_kernel(tc, x1, x2, out):
                                             identity=ident_f[:])
 
         def pe_xt(g):
-            m = at(g, XT_AT)
+            m = x_at(g)
             if m is not None:
                 bank[("x", g)] = psum.tile([P, 2, NB, P], BF16, tag="p", name="xt_ps", bufs=8)
                 for a in range(2):
@@ -214,7 +225,7 @@ def tile_mutualcrossattention_t_kernel(tc, x1, x2, out):
         def column_minima(g):
             for h in range(2):
                 m = at(g, LOW_AT[h])
-                if m is not None and mode(m) == 1:
+                if m is not None and mode(m) > 0:
                     nc.vector.tensor_reduce(out=low[:, 1, m, 2 * h:2 * h + 2], in_=bank[("low", m, h)][:].rearrange("p u k c -> p u (k c)"),
                                             axis=AX.X, op=ALU.min)
             m = at(g, LOW_AT[0])
@@ -222,21 +233,21 @@ def tile_mutualcrossattention_t_kernel(tc, x1, x2, out):
                 nc.vector.tensor_reduce(out=low[:, 1, m, :], in_=bank[("low", m, 0)][:], axis=AX.X, op=ALU.min)
 
         def mode(m):
-            return 1 if G_LO <= m < G_HI and m % G_EVERY != G_EVERY - 1 else 0
+            return 0 if not (G_LO <= m < G_HI) else (2 if m % G_EVERY != G_EVERY - 1 else 1)
 
         def x_copy(g):
-            m = at(g, XT_AT)
+            m = x_at(g)
             if m is not None and m >= X_ON_S and m % X_EVERY != 1:
                 do_x_copy(g, m, nc.vector.tensor_copy)
 
         def x_copy_s(g):
-            m = at(g, XT_AT)
+            m = x_at(g)
             if m is not None and not (m >= X_ON_S and m % X_EVERY != 1):
                 do_x_copy(g, m, nc.scalar.copy)
 
         def do_x_copy(g, m, copy):
             if True:
-                xT[m] = three.tile([P, 2, L], BF16, name="xT")
+                xT[m] = six.tile([P, 2, L], BF16, name="xT")
                 copy(out=xT[m][:], in_=bank[("x", g)][:].rearrange("p a t m -> p a (t m)"))
 
         def copies(g):
@@ -302,12 +313,11 @@ def tile_mutualcrossattention_t_kernel(tc, x1, x2, out):
                 xg[m] = one.tile([P, 2, D, NB], BF16, name="xg", align_bytes=64)
                 nc.gpsimd.tensor_scalar(out=xg[m][:], in0=xn[:, m].rearrange("p a t d -> p a d t"),
                                         scalar1=1.0, scalar2=0.0, op0=ALU.mult, op1=ALU.add)
-            m = at(g, GAP_AT)
-            if m is not None and mode(m) == 1:
-                nc.gpsimd.tensor_tensor(out=least[m][:, 0, :], in0=neg[m][:, 0, :], in1=neg[m][:, 1, :], op=ALU.subtract)
-                nc.gpsimd.tensor_scalar(out=least[m][:, 0, :], in0=least[m][:, 0, :], scalar1=0.0, scalar2=-BIG,
-                                        op0=ALU.min, op1=ALU.max)
-                nc.gpsimd.tensor_tensor(out=least[m][:, 0, :], in0=least[m][:, 0, :], in1=neg[m][:, 1, :], op=ALU.add)
+            for k in (1, 0):
+                m = at(g, GAP_AT[k])
+                if m is not None and (mode(m) == 2 or mode(m) == 1 and k == 0):
+                    nc.gpsimd.tensor_tensor(out=least[m][:, k, :], in0=neg[m][:, 2 * k, :], in1=neg[m][:, 2 * k + 1, :], op=ALU.subtract)
+                    nc.gpsimd.tensor_scalar(out=least[m][:, k, :], in0=least[m][:, k, :], scalar1=0.0, scalar2=-BIG, op0=ALU.min, op1=ALU.max)
 
         ctx.enter_context(tc.manual_schedule())
         for g in range(XT_AT, LAST + 1):

@@ -18,31 +18,33 @@ NB = L // P
 SCALE = 1.0 / (D ** 0.5)
 FLOPS = 3 * 2 * B * L * L * D
 
-XT_AT = -5
-XT_LAG = -100
-XG_AT = 4
-XQ_AT = 8
-GAP_AT = (2,4,)
-G_LO = 1
-G_HI = 16
+XT_AT = -7
+XT_LAG = -93
+XG_AT = 3
+XQ_AT = 6
+GAP_AT = (5,12,)
+G_MODE = 3
+G_LO = 2
+G_HI = 15
 G_EVERY = 1
-LOW_AT = (5,7,)
-EXP_AT = (1,6,)
-ET_AT = ((4,6,),(9,11,),)
-Q_AT = (8,12,)
-RCP_AT = 7
-MX_AT = (11,17,)
-END_Q_AT = (10,15,)
-END_MX_AT = (12,18,)
-LAST = NB * (B - 1) + max(MX_AT[1] + 1, END_MX_AT[1])
-PIECES = ((0, 1), (2, 3))
+LOW_AT = (6,-7,)
+EXP_AT = (1,7,)
+ET_AT = ((6,6,),(11,13,),)
+Q_AT = (10,14,)
+RCP_AT = 9
+MX_AT = (11,18,)
+END_Q_AT = (14,14,15,)
+END_MX_AT = (16,16,17,)
+LAST = NB * (B - 1) + max(MX_AT[1] + 1, max(END_MX_AT))
+PIECES = ((0, 1), (2,), (3,))
+FINE_END = True
 N_WARM = 3
 S_BUFS = 3
 BIG = 3.0e38
-ORDER = "cmCxXOeQVylRGtAELB"
+ORDER = "cRemCExyVlQOtXALGB"
 E_ON_V = 100
-X_ON_S = 3
-X_EVERY = 6
+X_ON_S = 4
+X_EVERY = 3
 MX_INSIDE = False
 ST_BUFS = 2
 ET_BUFS = 1
@@ -119,7 +121,7 @@ def tile_mutualcrossattention_t_kernel(tc, x1, x2, out):
         def pe_low(g):
             for h in range(2):
                 m = at(g, LOW_AT[h])
-                if m is not None and mode(m) > 0:
+                if m is not None and mode(m) in (1, 2):
                     bank[("low", m, h)] = psum.tile([P, 2, 2, P], F32, tag="p", name="low_ps", bufs=8)
                     for u in range(2):
                         cols = slice((2 * h + u) * P, (2 * h + u + 1) * P)
@@ -130,6 +132,12 @@ def tile_mutualcrossattention_t_kernel(tc, x1, x2, out):
                             else:
                                 nc.tensor.transpose(out=bank[("low", m, h)][:, u, k, :], in_=least[m][:, k, cols], identity=ident_f[:])
             m = at(g, LOW_AT[0])
+            if m is not None and mode(m) == 3:
+                bank[("low", m, 0)] = psum.tile([P, NB, P], F32, tag="p", name="low_ps", bufs=8)
+                for u in range(NB):
+                    cols = slice(u * P, (u + 1) * P)
+                    nc.tensor.matmul(out=bank[("low", m, 0)][:, u, :], lhsT=least[m][:, 1, cols], rhs=ident_f[:], start=True, stop=False, is_transpose=True)
+                    nc.tensor.matmul(out=bank[("low", m, 0)][:, u, :], lhsT=least[m][:, 0, cols], rhs=ident_f[:], start=False, stop=True, is_transpose=True)
             if m is not None and mode(m) == 0:
                 bank[("low", m, 0)] = psum.tile([P, NB, P], F32, tag="p", name="low_ps", bufs=8)
                 for u in range(NB):
@@ -146,11 +154,18 @@ def tile_mutualcrossattention_t_kernel(tc, x1, x2, out):
 
         def pe_et(g):
             for side, h, m in halves(g):
-                bank[("et", g)] = psum.tile([P, 2, 2, P], F32, tag="p", name="et_ps", bufs=8)
+                if FINE_END and (side, m, h) == (1, B - 1, 1):
+                    for r in range(2):
+                        bank[("et", g, r)] = psum.tile([P, 2, P], F32, tag="p", name="et_ps", bufs=8)
+                        for u in range(2):
+                            nc.tensor.transpose(out=bank[("et", g, r)][:, u, :], in_=ee[(side, m)][:, 2 * h + r, :].bitcast(F32)[:, u * P:(u + 1) * P],
+                                                identity=ident_f[:])
+                    continue
+                bank[("et", side, m, h)] = psum.tile([P, 2, 2, P], F32, tag="p", name="et_ps", bufs=8)
                 for r in range(2):
                     pairs = ee[(side, m)][:, 2 * h + r, :].bitcast(F32)
                     for u in range(2):
-                        nc.tensor.transpose(out=bank[("et", g)][:, r, u, :], in_=pairs[:, u * P:(u + 1) * P],
+                        nc.tensor.transpose(out=bank[("et", side, m, h)][:, r, u, :], in_=pairs[:, u * P:(u + 1) * P],
                                             identity=ident_f[:])
 
         def pe_xt(g):
@@ -225,15 +240,15 @@ def tile_mutualcrossattention_t_kernel(tc, x1, x2, out):
         def column_minima(g):
             for h in range(2):
                 m = at(g, LOW_AT[h])
-                if m is not None and mode(m) > 0:
+                if m is not None and mode(m) in (1, 2):
                     nc.vector.tensor_reduce(out=low[:, 1, m, 2 * h:2 * h + 2], in_=bank[("low", m, h)][:].rearrange("p u k c -> p u (k c)"),
                                             axis=AX.X, op=ALU.min)
             m = at(g, LOW_AT[0])
-            if m is not None and mode(m) == 0:
+            if m is not None and mode(m) in (0, 3):
                 nc.vector.tensor_reduce(out=low[:, 1, m, :], in_=bank[("low", m, 0)][:], axis=AX.X, op=ALU.min)
 
         def mode(m):
-            return 0 if not (G_LO <= m < G_HI) else (2 if m % G_EVERY != G_EVERY - 1 else 1)
+            return 0 if not (G_LO <= m < G_HI) else (3 if G_MODE == 3 else (2 if m % G_EVERY != G_EVERY - 1 else 1))
 
         def x_copy(g):
             m = x_at(g)
@@ -263,7 +278,10 @@ def tile_mutualcrossattention_t_kernel(tc, x1, x2, out):
                 if mode(m) == 0 and t > 0:
                     nc.vector.scalar_tensor_tensor(out=least[m][:, 0, :], in0=bank[("s", g)][:], scalar=-SCALE,
                                                    in1=neg[m][:, 0, :] if t == 1 else least[m][:, 0, :], op0=ALU.mult, op1=ALU.min)
-                if mode(m) == 1 and t == 3:
+                if mode(m) == 3 and t == 1:
+                    nc.vector.scalar_tensor_tensor(out=least[m][:, 0, :], in0=bank[("s", g)][:], scalar=-SCALE,
+                                                   in1=neg[m][:, 0, :], op0=ALU.mult, op1=ALU.min)
+                if mode(m) in (1, 3) and t == 3:
                     nc.vector.scalar_tensor_tensor(out=least[m][:, 1, :], in0=bank[("s", g)][:], scalar=-SCALE,
                                                    in1=neg[m][:, 2, :], op0=ALU.mult, op1=ALU.min)
 
@@ -286,8 +304,12 @@ def tile_mutualcrossattention_t_kernel(tc, x1, x2, out):
             for side, h, m in halves(g):
                 if h == 0:
                     grouped[(side, m)] = two.tile([P, NB, P, NB], BF16, name="grouped%d" % side, align_bytes=64)
+                if FINE_END and (side, m, h) == (1, B - 1, 1):
+                    for r in range(2):
+                        copy(out=grouped[(side, m)][:, 2 * h + r].bitcast(F32), in_=bank[("et", g, r)][:].rearrange("p u m -> p m u"))
+                    continue
                 copy(out=grouped[(side, m)][:, 2 * h:2 * h + 2].bitcast(F32),
-                     in_=bank[("et", g)][:].rearrange("p r u m -> p r m u"))
+                     in_=bank[("et", side, m, h)][:].rearrange("p r u m -> p r m u"))
 
         def s_a(g):
             exps(g, 0)
@@ -313,6 +335,10 @@ def tile_mutualcrossattention_t_kernel(tc, x1, x2, out):
                 xg[m] = one.tile([P, 2, D, NB], BF16, name="xg", align_bytes=64)
                 nc.gpsimd.tensor_scalar(out=xg[m][:], in0=xn[:, m].rearrange("p a t d -> p a d t"),
                                         scalar1=1.0, scalar2=0.0, op0=ALU.mult, op1=ALU.add)
+            m = at(g, GAP_AT[0])
+            if m is not None and mode(m) == 3:
+                nc.gpsimd.tensor_tensor(out=least[m][:, 0, :], in0=least[m][:, 0, :], in1=least[m][:, 1, :], op=ALU.subtract)
+                nc.gpsimd.tensor_scalar(out=least[m][:, 0, :], in0=least[m][:, 0, :], scalar1=0.0, scalar2=-BIG, op0=ALU.min, op1=ALU.max)
             for k in (1, 0):
                 m = at(g, GAP_AT[k])
                 if m is not None and (mode(m) == 2 or mode(m) == 1 and k == 0):

@@ -19,32 +19,36 @@ SCALE = 1.0 / (D ** 0.5)
 FLOPS = 3 * 2 * B * L * L * D
 
 XT_AT = -7
-XT_LAG = -93
-XG_AT = 3
+XT_LAG = -97
+XG_AT = 5
 XQ_AT = 6
-GAP_AT = (5,12,)
-G_MODE = 3
-G_LO = 2
+GAP_AT = (5,11,)
+G_MODE = 1
+G2_ORDER = (0,1,)
+GAP2_AT = (3,5,)
+LOW2_AT = (6,7,)
+G_LO = 1
 G_HI = 15
 G_EVERY = 1
-LOW_AT = (6,-7,)
+LOW_AT = (6,-8,)
 EXP_AT = (1,7,)
 ET_AT = ((6,6,),(11,13,),)
 Q_AT = (10,14,)
 RCP_AT = 9
-MX_AT = (11,18,)
-END_Q_AT = (14,14,15,)
-END_MX_AT = (16,16,17,)
+MX_AT = (12,20,)
+END_Q_AT = (15,16,17,)
+END_MX_AT = (18,18,19,)
 LAST = NB * (B - 1) + max(MX_AT[1] + 1, max(END_MX_AT))
 PIECES = ((0, 1), (2,), (3,))
 FINE_END = True
 N_WARM = 3
 S_BUFS = 3
 BIG = 3.0e38
-ORDER = "cRemCExyVlQOtXALGB"
+ORDER = "ceVCmxtGORQEylLXAB"
 E_ON_V = 100
-X_ON_S = 4
-X_EVERY = 3
+X_ON_S = 3
+X_EVERY = 2
+X_V = (0,)
 MX_INSIDE = False
 ST_BUFS = 2
 ET_BUFS = 1
@@ -120,7 +124,7 @@ def tile_mutualcrossattention_t_kernel(tc, x1, x2, out):
 
         def pe_low(g):
             for h in range(2):
-                m = at(g, LOW_AT[h])
+                m = at(g, LOW2_AT[h])
                 if m is not None and mode(m) in (1, 2):
                     bank[("low", m, h)] = psum.tile([P, 2, 2, P], F32, tag="p", name="low_ps", bufs=8)
                     for u in range(2):
@@ -239,7 +243,7 @@ def tile_mutualcrossattention_t_kernel(tc, x1, x2, out):
 
         def column_minima(g):
             for h in range(2):
-                m = at(g, LOW_AT[h])
+                m = at(g, LOW2_AT[h])
                 if m is not None and mode(m) in (1, 2):
                     nc.vector.tensor_reduce(out=low[:, 1, m, 2 * h:2 * h + 2], in_=bank[("low", m, h)][:].rearrange("p u k c -> p u (k c)"),
                                             axis=AX.X, op=ALU.min)
@@ -248,16 +252,16 @@ def tile_mutualcrossattention_t_kernel(tc, x1, x2, out):
                 nc.vector.tensor_reduce(out=low[:, 1, m, :], in_=bank[("low", m, 0)][:], axis=AX.X, op=ALU.min)
 
         def mode(m):
-            return 0 if not (G_LO <= m < G_HI) else (3 if G_MODE == 3 else (2 if m % G_EVERY != G_EVERY - 1 else 1))
+            return 0 if not (G_LO <= m < G_HI) else (2 if m % G_EVERY == 1 else 3)
 
         def x_copy(g):
             m = x_at(g)
-            if m is not None and m >= X_ON_S and m % X_EVERY != 1:
+            if m is not None and m >= X_ON_S and m % X_EVERY in X_V:
                 do_x_copy(g, m, nc.vector.tensor_copy)
 
         def x_copy_s(g):
             m = x_at(g)
-            if m is not None and not (m >= X_ON_S and m % X_EVERY != 1):
+            if m is not None and not (m >= X_ON_S and m % X_EVERY in X_V):
                 do_x_copy(g, m, nc.scalar.copy)
 
         def do_x_copy(g, m, copy):
@@ -339,8 +343,8 @@ def tile_mutualcrossattention_t_kernel(tc, x1, x2, out):
             if m is not None and mode(m) == 3:
                 nc.gpsimd.tensor_tensor(out=least[m][:, 0, :], in0=least[m][:, 0, :], in1=least[m][:, 1, :], op=ALU.subtract)
                 nc.gpsimd.tensor_scalar(out=least[m][:, 0, :], in0=least[m][:, 0, :], scalar1=0.0, scalar2=-BIG, op0=ALU.min, op1=ALU.max)
-            for k in (1, 0):
-                m = at(g, GAP_AT[k])
+            for k in G2_ORDER:
+                m = at(g, GAP2_AT[k])
                 if m is not None and (mode(m) == 2 or mode(m) == 1 and k == 0):
                     nc.gpsimd.tensor_tensor(out=least[m][:, k, :], in0=neg[m][:, 2 * k, :], in1=neg[m][:, 2 * k + 1, :], op=ALU.subtract)
                     nc.gpsimd.tensor_scalar(out=least[m][:, k, :], in0=least[m][:, k, :], scalar1=0.0, scalar2=-BIG, op0=ALU.min, op1=ALU.max)

from contextlib import ExitStack

import concourse.mybir as mybir
from concourse.masks import make_identity

FP8X4 = mybir.dt.float8_e4m3fn_x4
BF16 = mybir.dt.bfloat16
F32 = mybir.dt.float32
U32 = mybir.dt.uint32
U8 = mybir.dt.uint8
ALU = mybir.AluOpType
ACT = mybir.ActivationFunctionType
AX = mybir.AxisListType

B, L, D = 16, 512, 128
P = 128
NB = L // P
SCALE = 1.0 / (D ** 0.5)
FLOPS = 3 * 2 * B * L * L * D

XT_AT = -7
XT_LAG = -97
XG_AT = 5
XQ_AT = 6
GAP_AT = (5,11,)
G_MODE = 1
G2_ORDER = (0,1,)
GAP2_AT = (3,5,)
LOW2_AT = (6,7,)
G_LO = 1
G_HI = 15
G_EVERY = 1
LOW_AT = (6,-8,)
EXP_AT = (1,7,)
ET_AT = ((6,6,),(11,13,),)
Q_AT = (10,14,)
RCP_AT = 9
MX_AT = (12,20,)
END_Q_AT = (15,16,17,)
END_MX_AT = (18,18,19,)
LAST = NB * (B - 1) + max(MX_AT[1] + 1, max(END_MX_AT))
PIECES = ((0, 1), (2,), (3,))
FINE_END = True
N_WARM = 3
S_BUFS = 3
BIG = 3.0e38
ORDER = "ceVCmxtGORQEylLXAB"
E_ON_V = 100
X_ON_S = 3
X_EVERY = 2
X_V = (0,)
MX_INSIDE = False
ST_BUFS = 2
ET_BUFS = 1
O_BUFS = 2


def tile_mutualcrossattention_t_kernel(tc, x1, x2, out):
    nc = tc.nc
    with ExitStack() as ctx:
        keep = ctx.enter_context(tc.tile_pool(name="keep", bufs=1))
        one = keep
        two = ctx.enter_context(tc.tile_pool(name="two", bufs=2))
        three = ctx.enter_context(tc.tile_pool(name="three", bufs=3))
        six = ctx.enter_context(tc.tile_pool(name="six", bufs=6))
        four = ctx.enter_context(tc.tile_pool(name="four", bufs=4))
        psum = ctx.enter_context(tc.psum_pool(name="psum", bufs=2))

        idle = keep.tile([P, L], BF16, name="idle")
        nc.vector.memset(idle[:], 0.0)
        idle_ps = psum.tile([P, L], F32, tag="p", name="idle_ps", bufs=8)
        for i in range(N_WARM):
            nc.tensor.matmul(out=idle_ps[:], lhsT=idle[:, 0:P], rhs=idle[:], start=True, stop=True)

        xn = keep.tile([P, B, 2, NB, D], BF16, name="xn")
        cuts = [0, 1, 2, 4, 8, 16]
        for lo, hi in zip(cuts[:-1], cuts[1:]):
            nc.sync.dma_start(out=xn[:, lo:hi, 0], in_=x1[lo:hi].rearrange("b (p t) d -> p b t d", t=NB))
            nc.sync.dma_start(out=xn[:, lo:hi, 1], in_=x2[lo:hi].rearrange("b (p t) d -> p b t d", t=NB))

        ident_b = keep.tile([P, P], BF16, name="ident_b")
        make_identity(nc, ident_b[:])
        ident_f = keep.tile([P, P], F32, name="ident_f")
        make_identity(nc, ident_f[:])

        xw = keep.tile([P, B, 2 * D], U32, name="xw", align_bytes=64)
        xs = keep.tile([P, B, 2 * D], U8, name="xs", align_bytes=64)
        low = keep.tile([P, 2, B, NB], F32, name="low")
        sums = keep.tile([P, B, 2, NB], F32, name="sums")
        rcp = keep.tile([P, B, 2, NB], F32, name="rcp")

        xT, xg, neg, least, ee, grouped, words, planes, scaled, osb = {}, {}, {}, {}, {}, {}, {}, {}, {}, {}
        bank = {}

        def at(g, first):
            m, r = divmod(g - first, NB)
            return m if (r == 0 and 0 <= m < B) else None

        def x_at(g):
            found = [m for m in range(B) if (XT_AT if m == 0 else max(m - 1 + XT_LAG, XT_AT + 4 * m)) == g]
            return found[0] if found else None

        def split(g, first):
            m, q = divmod(g - first, NB)
            return (m, q) if 0 <= m < B else None

        def halves(g):
            return [(side, h, at(g, ET_AT[side][h])) for side in range(2) for h in range(2)
                    if at(g, ET_AT[side][h]) is not None]

        def by_halves(g, whole, halved):
            found = []
            for side in range(2):
                m = at(g, whole[side])
                if m is not None and (side, m) != (1, B - 1):
                    found.append((side, m, (0, 1, 2, 3)))
            for h in range(len(PIECES)):
                if g == NB * (B - 1) + halved[h]:
                    found.append((1, B - 1, PIECES[h]))
            return found

        def products(g):
            return by_halves(g, MX_AT, END_MX_AT)

        def pe_low(g):
            for h in range(2):
                m = at(g, LOW2_AT[h])
                if m is not None and mode(m) in (1, 2):
                    bank[("low", m, h)] = psum.tile([P, 2, 2, P], F32, tag="p", name="low_ps", bufs=8)
                    for u in range(2):
                        cols = slice((2 * h + u) * P, (2 * h + u + 1) * P)
                        for k in range(2):
                            if mode(m) == 2 or k == 0:
                                nc.tensor.matmul(out=bank[("low", m, h)][:, u, k, :], lhsT=neg[m][:, 2 * k + 1, cols], rhs=ident_f[:], start=True, stop=False, is_transpose=True)
                                nc.tensor.matmul(out=bank[("low", m, h)][:, u, k, :], lhsT=least[m][:, k, cols], rhs=ident_f[:], start=False, stop=True, is_transpose=True)
                            else:
                                nc.tensor.transpose(out=bank[("low", m, h)][:, u, k, :], in_=least[m][:, k, cols], identity=ident_f[:])
            m = at(g, LOW_AT[0])
            if m is not None and mode(m) == 3:
                bank[("low", m, 0)] = psum.tile([P, NB, P], F32, tag="p", name="low_ps", bufs=8)
                for u in range(NB):
                    cols = slice(u * P, (u + 1) * P)
                    nc.tensor.matmul(out=bank[("low", m, 0)][:, u, :], lhsT=least[m][:, 1, cols], rhs=ident_f[:], start=True, stop=False, is_transpose=True)
                    nc.tensor.matmul(out=bank[("low", m, 0)][:, u, :], lhsT=least[m][:, 0, cols], rhs=ident_f[:], start=False, stop=True, is_transpose=True)
            if m is not None and mode(m) == 0:
                bank[("low", m, 0)] = psum.tile([P, NB, P], F32, tag="p", name="low_ps", bufs=8)
                for u in range(NB):
                    nc.tensor.transpose(out=bank[("low", m, 0)][:, u, :], in_=least[m][:, 0, u * P:(u + 1) * P], identity=ident_f[:])

        def pe_st(g):
            st = split(g, EXP_AT[1])
            if st is not None:
                m, u = st
                bank[("st", g)] = psum.tile([P, L], F32, tag="p", name="st_ps", bufs=8)
                for t in range(NB):
                    nc.tensor.transpose(out=bank[("st", g)][:, t * P:(t + 1) * P],
                                        in_=neg[m][:, t, u * P:(u + 1) * P], identity=ident_f[:])

        def pe_et(g):
            for side, h, m in halves(g):
                if FINE_END and (side, m, h) == (1, B - 1, 1):
                    for r in range(2):
                        bank[("et", g, r)] = psum.tile([P, 2, P], F32, tag="p", name="et_ps", bufs=8)
                        for u in range(2):
                            nc.tensor.transpose(out=bank[("et", g, r)][:, u, :], in_=ee[(side, m)][:, 2 * h + r, :].bitcast(F32)[:, u * P:(u + 1) * P],
                                                identity=ident_f[:])
                    continue
                bank[("et", side, m, h)] = psum.tile([P, 2, 2, P], F32, tag="p", name="et_ps", bufs=8)
                for r in range(2):
                    pairs = ee[(side, m)][:, 2 * h + r, :].bitcast(F32)
                    for u in range(2):
                        nc.tensor.transpose(out=bank[("et", side, m, h)][:, r, u, :], in_=pairs[:, u * P:(u + 1) * P],
                                            identity=ident_f[:])

        def pe_xt(g):
            m = x_at(g)
            if m is not None:
                bank[("x", g)] = psum.tile([P, 2, NB, P], BF16, tag="p", name="xt_ps", bufs=8)
                for a in range(2):
                    for t in range(NB):
                        nc.tensor.transpose(out=bank[("x", g)][:, a, t, :], in_=xn[:, m, a, t, :], identity=ident_b[:])

        def pe_scores(g):
            hw = L // 2
            sc = split(g, 0)
            if sc is not None:
                m, t = sc
                bank[("s", g)] = psum.tile([P, L], F32, tag="p", name="s_ps", bufs=8)
                nc.tensor.matmul(out=bank[("s", g)][:, 0:hw], lhsT=xT[m][:, 0, t * P:(t + 1) * P],
                                 rhs=xT[m][:, 1, 0:hw], start=True, stop=True)
            if MX_INSIDE:
                pe_mx(g)
            if sc is not None:
                m, t = sc
                nc.tensor.matmul(out=bank[("s", g)][:, hw:L], lhsT=xT[m][:, 0, t * P:(t + 1) * P],
                                 rhs=xT[m][:, 1, hw:L], start=True, stop=True)

        def pe_m(g):
            if not MX_INSIDE:
                pe_mx(g)

        def pe_mx(g):
            for side, m, tiles in products(g):
                if tiles[0] == 0:
                    bank[("o", side, m)] = psum.tile([P, NB, D], F32, tag="p", name="acc", bufs=8)
                lo = (1 - side) * D
                for q in tiles:
                    nc.tensor.matmul_mx(out=bank[("o", side, m)][:, q, :],
                                        lhsT=words[(side, m)][:, q * P:(q + 1) * P].bitcast(FP8X4),
                                        lhsT_scale=planes[(side, m)][:, q * P:(q + 1) * P],
                                        rhs=xw[:, m, lo:lo + D].bitcast(FP8X4),
                                        rhs_scale=xs[:, m, lo:lo + D], start=True, stop=True)

        def scalings(g):
            for side, m, tiles in products(g):
                if side == 0:
                    scaled[m] = three.tile([P, NB, D], F32, name="scaled")
                    nc.vector.tensor_tensor(out=scaled[m][:], in0=bank[("o", 0, m)][:],
                                            in1=rcp[:, m, 0, :].unsqueeze(2).to_broadcast([P, NB, D]), op=ALU.mult)
                else:
                    if tiles[0] == 0:
                        osb[m] = three.tile([P, NB, D], F32, name="osb")
                    for q in tiles:
                        nc.vector.scalar_tensor_tensor(out=osb[m][:, q, :], in0=bank[("o", 1, m)][:, q, :],
                                                       scalar=rcp[:, m, 1, q:q + 1], in1=scaled[m][:, q, :],
                                                       op0=ALU.mult, op1=ALU.add)
                    lo, hi = tiles[0], tiles[-1] + 1
                    nc.sync.dma_start(out=out[m].rearrange("(p q) d -> p q d", q=NB)[:, lo:hi, :], in_=osb[m][:, lo:hi, :])

        def quantises(g):
            for side, m, tiles in by_halves(g, Q_AT, END_Q_AT):
                if tiles[0] == 0:
                    words[(side, m)] = three.tile([P, L], U32, name="words%d" % side, align_bytes=64)
                    planes[(side, m)] = three.tile([P, L], U8, name="planes%d" % side, align_bytes=64)
                lo, hi = tiles[0], tiles[-1] + 1
                nc.vector.quantize_mx(out=words[(side, m)][:, lo * P:hi * P].bitcast(FP8X4),
                                      scales=planes[(side, m)][:, lo * P:hi * P],
                                      in_=grouped[(side, m)][:, lo:hi].rearrange("p r m c -> p (r m c)"))
            m = at(g, XQ_AT)
            if m is not None:
                nc.vector.quantize_mx(out=xw[:, m, :].bitcast(FP8X4), scales=xs[:, m, :],
                                      in_=xg[m][:].rearrange("p a d t -> p (a d t)"))

        def column_minima(g):
            for h in range(2):
                m = at(g, LOW2_AT[h])
                if m is not None and mode(m) in (1, 2):
                    nc.vector.tensor_reduce(out=low[:, 1, m, 2 * h:2 * h + 2], in_=bank[("low", m, h)][:].rearrange("p u k c -> p u (k c)"),
                                            axis=AX.X, op=ALU.min)
            m = at(g, LOW_AT[0])
            if m is not None and mode(m) in (0, 3):
                nc.vector.tensor_reduce(out=low[:, 1, m, :], in_=bank[("low", m, 0)][:], axis=AX.X, op=ALU.min)

        def mode(m):
            return 0 if not (G_LO <= m < G_HI) else (2 if m % G_EVERY == 1 else 3)

        def x_copy(g):
            m = x_at(g)
            if m is not None and m >= X_ON_S and m % X_EVERY in X_V:
                do_x_copy(g, m, nc.vector.tensor_copy)

        def x_copy_s(g):
            m = x_at(g)
            if m is not None and not (m >= X_ON_S and m % X_EVERY in X_V):
                do_x_copy(g, m, nc.scalar.copy)

        def do_x_copy(g, m, copy):
            if True:
                xT[m] = six.tile([P, 2, L], BF16, name="xT")
                copy(out=xT[m][:], in_=bank[("x", g)][:].rearrange("p a t m -> p a (t m)"))

        def copies(g):
            e = split(g, 0)
            if e is not None:
                m, t = e
                if t == 0:
                    neg[m] = four.tile([P, NB, L], F32, name="neg0")
                nc.vector.tensor_scalar(out=neg[m][:, t, :], in0=bank[("s", g)][:], scalar1=-SCALE,
                                        scalar2=None, op0=ALU.mult, op1=ALU.min, accum_out=low[:, 0, m, t:t + 1])
                if t == 0:
                    least[m] = two.tile([P, 2, L], F32, name="least")
                if mode(m) == 0 and t > 0:
                    nc.vector.scalar_tensor_tensor(out=least[m][:, 0, :], in0=bank[("s", g)][:], scalar=-SCALE,
                                                   in1=neg[m][:, 0, :] if t == 1 else least[m][:, 0, :], op0=ALU.mult, op1=ALU.min)
                if mode(m) == 3 and t == 1:
                    nc.vector.scalar_tensor_tensor(out=least[m][:, 0, :], in0=bank[("s", g)][:], scalar=-SCALE,
                                                   in1=neg[m][:, 0, :], op0=ALU.mult, op1=ALU.min)
                if mode(m) in (1, 3) and t == 3:
                    nc.vector.scalar_tensor_tensor(out=least[m][:, 1, :], in0=bank[("s", g)][:], scalar=-SCALE,
                                                   in1=neg[m][:, 2, :], op0=ALU.mult, op1=ALU.min)

        def reciprocals(g):
            m, r = divmod(g - RCP_AT, NB)
            if r == 0 and 0 <= m <= B:
                lo, hi = max(0, 2 * NB * m - NB), min(2 * NB * B, 2 * NB * m + NB)
                nc.vector.reciprocal(out=rcp[:].rearrange("p b s t -> p (b s t)")[:, lo:hi],
                                     in_=sums[:].rearrange("p b s t -> p (b s t)")[:, lo:hi])

        def s_copy(g):
            if g < E_ON_V:
                e_copy(g, nc.scalar.copy)

        def v_copy(g):
            if g >= E_ON_V:
                e_copy(g, nc.vector.tensor_copy)

        def e_copy(g, copy):
            for side, h, m in halves(g):
                if h == 0:
                    grouped[(side, m)] = two.tile([P, NB, P, NB], BF16, name="grouped%d" % side, align_bytes=64)
                if FINE_END and (side, m, h) == (1, B - 1, 1):
                    for r in range(2):
                        copy(out=grouped[(side, m)][:, 2 * h + r].bitcast(F32), in_=bank[("et", g, r)][:].rearrange("p u m -> p m u"))
                    continue
                copy(out=grouped[(side, m)][:, 2 * h:2 * h + 2].bitcast(F32),
                     in_=bank[("et", side, m, h)][:].rearrange("p r u m -> p r m u"))

        def s_a(g):
            exps(g, 0)

        def s_b(g):
            exps(g, 1)

        def exps(g, side):
            if True:
                e = split(g, EXP_AT[side])
                if e is not None:
                    m, t = e
                    if t == 0:
                        ee[(side, m)] = three.tile([P, NB, L], BF16, name="ee%d" % side)
                    nc.scalar.activation(out=ee[(side, m)][:, t, :].rearrange("p (u q e) -> p u q e", u=2, e=2),
                                         in_=(neg[m][:, t, :] if side == 0 else bank[("st", g)][:]).rearrange("p (u e q) -> p u q e", u=2, e=2),
                                         func=ACT.Exp, bias=low[:, side, m, t:t + 1], scale=-1.0,
                                         accum_out=sums[:, m, side, t:t + 1])

        def gpsimd(g):
            m = at(g, XG_AT)
            if m is not None:
                xg[m] = one.tile([P, 2, D, NB], BF16, name="xg", align_bytes=64)
                nc.gpsimd.tensor_scalar(out=xg[m][:], in0=xn[:, m].rearrange("p a t d -> p a d t"),
                                        scalar1=1.0, scalar2=0.0, op0=ALU.mult, op1=ALU.add)
            m = at(g, GAP_AT[0])
            if m is not None and mode(m) == 3:
                nc.gpsimd.tensor_tensor(out=least[m][:, 0, :], in0=least[m][:, 0, :], in1=least[m][:, 1, :], op=ALU.subtract)
                nc.gpsimd.tensor_scalar(out=least[m][:, 0, :], in0=least[m][:, 0, :], scalar1=0.0, scalar2=-BIG, op0=ALU.min, op1=ALU.max)
            for k in G2_ORDER:
                m = at(g, GAP2_AT[k])
                if m is not None and (mode(m) == 2 or mode(m) == 1 and k == 0):
                    nc.gpsimd.tensor_tensor(out=least[m][:, k, :], in0=neg[m][:, 2 * k, :], in1=neg[m][:, 2 * k + 1, :], op=ALU.subtract)
                    nc.gpsimd.tensor_scalar(out=least[m][:, k, :], in0=least[m][:, k, :], scalar1=0.0, scalar2=-BIG, op0=ALU.min, op1=ALU.max)

        ctx.enter_context(tc.manual_schedule())
        for g in range(XT_AT, LAST + 1):
            tasks = {"e": pe_et, "x": pe_xt, "c": pe_scores, "l": pe_low, "t": pe_st, "m": pe_m,
                     "C": copies, "L": column_minima, "X": x_copy, "O": scalings, "R": reciprocals, "Q": quantises,
                     "E": s_copy, "A": s_a, "B": s_b, "G": gpsimd, "y": x_copy_s, "V": v_copy}
            for k in ORDER:
                tasks[k](g)
